import numpy as np
import ml_dtypes


def mxq(x, axis, fmt="e4m3"):
    dtype, down = {"e4m3": (ml_dtypes.float8_e4m3fn, 7), "e5m2": (ml_dtypes.float8_e5m2, 14)}[fmt]
    v = np.moveaxis(np.asarray(x, np.float32).astype(ml_dtypes.bfloat16).astype(np.float64), axis, -1)
    blocks = v.reshape(v.shape[:-1] + (-1, 32))
    amax = np.abs(blocks).max(-1, keepdims=True)
    byte = np.maximum(np.where(amax > 0, np.frexp(amax)[1] - 1 + 127, 0) - down, 1)
    scale = np.exp2(byte - 127.0)
    codes = (blocks / scale).astype(np.float32).astype(dtype).astype(np.float64)
    return np.moveaxis((codes * scale).reshape(v.shape), -1, axis)


WIDE = False


def mx_kscale(k):
    if not WIDE:
        return np.ones(k)
    levels = np.array([10, -10, 5, -5, 0])
    a = np.random.permutation(np.resize(levels, k // 512 * 4)).reshape(k // 512, 4)
    idx = np.arange(k)
    return np.exp2(a[idx // 512, idx % 128 // 32])


BF16 = ml_dtypes.bfloat16


def bf(x):
    return np.asarray(x, np.float32).astype(BF16)


def f64(x):
    return np.asarray(x).astype(np.float64)


B, L, X, E, Y = 4, 1024, 3, 128, 3
XS = X - 1
PAIRS = [(x, y) for x in range(1, X) for y in range(min(x + 1, Y))]
P = len(PAIRS)
SCALE = 1.0 / np.sqrt(E)


def setup_inputs():
    a = np.log2(mx_kscale(L))
    a = a - a.max()
    g = np.where(a < 0, 0.25, 1.0) * np.exp2(-a)
    q = np.random.standard_normal((B, L, XS, E))
    q[..., 0] = 1.0
    k = np.random.standard_normal((B, P, L, E))
    r = np.random.standard_normal((B, P, L, E)) * 6.0 / np.sqrt(L)
    for p, (_, y) in enumerate(PAIRS):
        if y == 0:
            k[:, p, :, 0] += a * np.log(2.0) / SCALE
            r[:, p] *= g[:, None]
    return {"q_plus": bf(q), "key_plus": bf(k), "retrieval": bf(r)}


def reference(q_plus, key_plus, retrieval):
    q, k, r = f64(q_plus), f64(key_plus), f64(retrieval)
    heads = []
    for x in range(1, X):
        ps = [p for p, (i, _) in enumerate(PAIRS) if i == x]
        s = [(q[:, :, x - 1, :] @ k[:, p].transpose(0, 2, 1)) * SCALE for p in ps]
        top = np.maximum.reduce(s)
        e = [np.exp(v - top) for v in s]
        den = sum(e)
        heads.append(sum((mxq(ei / den, 2, "e4m3") @ mxq(r[:, p], 1, "e4m3")) for ei, p in zip(e, ps)))
    return np.stack(heads, 2)

@@ -1,0 +1,326 @@
+import math
+from contextlib import ExitStack
+
+import concourse.mybir as mybir
+from concourse.masks import make_identity
+
+F32 = mybir.dt.float32
+BF16 = mybir.dt.bfloat16
+U32 = mybir.dt.uint32
+U8 = mybir.dt.uint8
+FP8X4 = mybir.dt.float8_e4m3fn_x4
+FUNC = mybir.ActivationFunctionType
+ALU = mybir.AluOpType
+
+BATCHES = 4
+LENGTH = 1024
+CHANNELS = 128
+N_PAIRS = 5
+HEAD1_PAIRS = (0, 1)
+HEAD2_PAIRS = (2, 3, 4)
+SCALE = 1.0 / math.sqrt(CHANNELS)
+
+P = 128
+PACK = 4
+PASSES = LENGTH // (P * PACK)
+QUERY_TILES = LENGTH // P
+BANK = P * PACK
+STEP = PASSES * BANK
+STEPS = BATCHES * QUERY_TILES
+CHUNK = 4
+SCORES_AHEAD = 5
+SHARE_AHEAD = 4
+LOAD_AHEAD = 2
+TINY = 2.0**-60
+
+FLOPS = 2 * 2 * BATCHES * N_PAIRS * LENGTH * LENGTH * CHANNELS
+
+
+def tile_anomalyattention_pa_t_kernel(tc, q_plus, key_plus, retrieval, out):
+    nc = tc.nc
+    stack = ExitStack()
+    with stack:
+        sbuf = stack.enter_context(tc.tile_pool(name="sbuf", bufs=1))
+        psum = stack.enter_context(tc.psum_pool(name="psum", bufs=1))
+        stack.enter_context(tc.manual_schedule())
+
+        def sb(shape, dtype, tag, bufs):
+            return sbuf.tile(shape, dtype, name=tag, tag=tag, bufs=bufs, align_bytes=64)
+
+        def by_query(bank):
+            return bank[:].rearrange("p t l -> p l t")
+
+        def half(tile, g):
+            return tile[:, g * BANK : (g + 1) * BANK].rearrange("p (l t) -> p l t", t=PACK)
+
+        identity = sb([P, P], BF16, "identity", 1)
+        make_identity(nc, identity[:])
+        tiny = sb([P, 1], F32, "tiny", 1)
+        nc.vector.memset(tiny[:], TINY)
+
+        live = {}
+
+        def load_keys(batch, pair):
+            raw = sb([P, PASSES, PACK, CHANNELS], BF16, "key_raw", LOAD_AHEAD + 1)
+            nc.sync.dma_start(
+                out=raw[:],
+                in_=key_plus[batch, pair].rearrange("(g p t) e -> p g t e", g=PASSES, t=PACK),
+            )
+            live["key_raw", batch, pair] = raw
+
+        def transpose_keys(batch, pair):
+            raw = live["key_raw", batch, pair]
+            flipped = psum.tile([P, PASSES, PACK, P], BF16, name="flipped", tag="flipped", bufs=1)
+            for g in range(PASSES):
+                for t in range(PACK):
+                    nc.tensor.transpose(out=flipped[:, g, t, :], in_=raw[:, g, t, :], identity=identity[:])
+            keys_t = sb([P, PASSES, PACK, P], BF16, "keys_t%d" % pair, 2)
+            nc.vector.tensor_copy(out=keys_t[:], in_=flipped[:])
+            live["keys_t", batch, pair] = keys_t
+
+        def load_queries(batch):
+            raw = sb([P, QUERY_TILES, 2, CHANNELS], BF16, "query_raw", 1)
+            nc.sync.dma_start(
+                out=raw[:], in_=q_plus[batch].rearrange("(p i) x e -> p i x e", i=QUERY_TILES)
+            )
+            live["query_raw", batch] = raw
+
+        def transpose_queries(batch, head):
+            raw = live["query_raw", batch]
+            flipped = psum.tile([P, QUERY_TILES, P], BF16, name="flipped", tag="flipped", bufs=1)
+            for i in range(QUERY_TILES):
+                nc.tensor.transpose(out=flipped[:, i, :], in_=raw[:, i, head, :], identity=identity[:])
+            queries_t = sb([P, QUERY_TILES, P], BF16, "queries_t%d" % head, 2)
+            nc.vector.tensor_copy(out=queries_t[:], in_=flipped[:])
+            live["queries_t", batch, head] = queries_t
+            if head == 0:
+                minus_t = sb([P, QUERY_TILES, P], BF16, "minus_queries_t", 2)
+                nc.vector.tensor_scalar_mul(out=minus_t[:], in0=flipped[:], scalar1=-1.0)
+                live["minus_queries_t", batch] = minus_t
+
+        def load_values(batch, pair):
+            raw = sb([P, PASSES, PACK, CHANNELS], BF16, "value_raw", LOAD_AHEAD + 1)
+            nc.sync.dma_start(
+                out=raw[:],
+                in_=retrieval[batch, pair].rearrange("(g p t) e -> p g t e", g=PASSES, t=PACK),
+            )
+            live["value_raw", batch, pair] = raw
+
+        def group_values(batch, pair):
+            raw = live["value_raw", batch, pair]
+            grouped = sb([P, PASSES, CHANNELS, PACK], BF16, "value_grouped", 2)
+            nc.vector.tensor_copy(out=grouped[:], in_=raw[:].rearrange("p g t e -> p g e t"))
+            live["value_grouped", batch, pair] = grouped
+
+        def quantise_values(batch, pair):
+            grouped = live["value_grouped", batch, pair]
+            if pair == 0:
+                live["value_codes", batch] = sb([P, N_PAIRS, PASSES * CHANNELS], U32, "value_codes", 2)
+                live["value_scales", batch] = sb([P, N_PAIRS, PASSES * CHANNELS], U8, "value_scales", 2)
+            nc.vector.quantize_mx(
+                out=live["value_codes", batch][:, pair, :].bitcast(FP8X4),
+                scales=live["value_scales", batch][:, pair, :],
+                in_=grouped[:].rearrange("p g e t -> p (g e t)"),
+            )
+
+        def score_bank(tag, batch, i, g, terms):
+            bank = psum.tile([P, PACK, P], F32, name=tag, tag=tag, bufs=3)
+            for t in range(PACK):
+                for j, (keys_t, queries_t) in enumerate(terms):
+                    nc.tensor.matmul(
+                        out=bank[:, t, :],
+                        lhsT=keys_t[:, g, t, :],
+                        rhs=queries_t[:, i, :],
+                        start=(j == 0),
+                        stop=(j == len(terms) - 1),
+                    )
+            return bank
+
+        def quantise_series(name, step):
+            series = live[name, step]
+            codes = sb([P, PASSES * P], U32, name + "_codes", 3)
+            scales = sb([P, PASSES * P], U8, name + "_scales", 3)
+            nc.vector.quantize_mx(out=codes[:].bitcast(FP8X4), scales=scales[:], in_=series[:])
+            live[name + "_codes", step] = codes
+            live[name + "_scales", step] = scales
+
+        def head1_series(step):
+            batch, i = divmod(step, QUERY_TILES)
+            first = sb([P, STEP], BF16, "h1y0", 2)
+            second = sb([P, STEP], BF16, "h1y1", 2)
+            for g in range(PASSES):
+                gap = score_bank(
+                    "gap", batch, i, g,
+                    [
+                        (live["keys_t", batch, 0], live["queries_t", batch, 0]),
+                        (live["keys_t", batch, 1], live["minus_queries_t", batch]),
+                    ],
+                )
+                nc.scalar.activation(out=half(first, g), in_=by_query(gap), func=FUNC.Sigmoid, scale=SCALE)
+                nc.scalar.activation(out=half(second, g), in_=by_query(gap), func=FUNC.Sigmoid, scale=-SCALE)
+            live["h1y0", step] = first
+            live["h1y1", step] = second
+
+        def head2_differences(step):
+            batch, i = divmod(step, QUERY_TILES)
+            queries_t = live["queries_t", batch, 1]
+            d12 = sb([P, STEP], F32, "d12", SCORES_AHEAD + 1)
+            d01 = sb([P, STEP], F32, "d01", SCORES_AHEAD + 1)
+            for g in range(PASSES):
+                s1 = score_bank("score", batch, i, g, [(live["keys_t", batch, 3], queries_t)])
+                s2 = score_bank("score", batch, i, g, [(live["keys_t", batch, 4], queries_t)])
+                s0 = score_bank("score", batch, i, g, [(live["keys_t", batch, 2], queries_t)])
+                a1 = sb([P, P, PACK], F32, "a1", 2)
+                nc.vector.tensor_scalar_mul(out=a1[:], in0=by_query(s1), scalar1=SCALE)
+                nc.vector.scalar_tensor_tensor(
+                    out=half(d12, g), in0=by_query(s2), scalar=-SCALE, in1=a1[:], op0=ALU.mult, op1=ALU.add
+                )
+                nc.vector.scalar_tensor_tensor(
+                    out=half(d01, g), in0=by_query(s0), scalar=SCALE, in1=a1[:], op0=ALU.mult, op1=ALU.subtract
+                )
+            live["d12", step] = d12
+            live["d01", step] = d01
+
+        def head2_share1(step):
+            share1 = sb([P, STEP], F32, "share1", SHARE_AHEAD + 2)
+            nc.scalar.activation(out=share1[:], in_=live["d12", step][:], func=FUNC.Sigmoid)
+            live["share1", step] = share1
+
+        def head2_log_share1(step):
+            logit = sb([P, STEP], F32, "logit", CHUNK)
+            nc.scalar.activation(out=logit[:], in_=live["share1", step][:], func=FUNC.Ln, bias=tiny[:])
+            live["logit", step] = logit
+
+        def head2_logit(step):
+            logit = live["logit", step]
+            nc.vector.tensor_tensor(out=logit[:], in0=live["d12", step][:], in1=logit[:], op=ALU.min)
+            nc.vector.tensor_tensor(out=logit[:], in0=live["d01", step][:], in1=logit[:], op=ALU.add)
+
+        def head2_share2(step):
+            share2 = sb([P, STEP], F32, "share2", 2)
+            nc.scalar.activation(out=share2[:], in_=live["d12", step][:], func=FUNC.Sigmoid, scale=-1.0)
+            live["share2", step] = share2
+
+        def head2_split(step):
+            logit = live["logit", step]
+            y0 = sb([P, STEP], BF16, "h2y0", 3)
+            rest = sb([P, STEP], F32, "rest", 2)
+            nc.scalar.activation(out=y0[:], in_=logit[:], func=FUNC.Sigmoid)
+            nc.scalar.activation(out=rest[:], in_=logit[:], func=FUNC.Sigmoid, scale=-1.0)
+            live["h2y0", step] = y0
+            live["rest", step] = rest
+
+        def head2_products(step):
+            rest = live["rest", step]
+            y1 = sb([P, STEP], BF16, "h2y1", 2)
+            y2 = sb([P, STEP], BF16, "h2y2", 2)
+            nc.gpsimd.tensor_tensor(out=y1[:], in0=rest[:], in1=live["share1", step][:], op=ALU.mult)
+            nc.gpsimd.tensor_tensor(out=y2[:], in0=rest[:], in1=live["share2", step][:], op=ALU.mult)
+            live["h2y1", step] = y1
+            live["h2y2", step] = y2
+
+        def multiply(step):
+            batch = step // QUERY_TILES
+            product = psum.tile([P, 2, CHANNELS], F32, name="product", tag="product", bufs=1)
+            heads = (
+                (("h1y0", "h1y1"), HEAD1_PAIRS),
+                (("h2y0", "h2y1", "h2y2"), HEAD2_PAIRS),
+            )
+            for x, (names, pairs) in enumerate(heads):
+                last = len(names) * PASSES - 1
+                for y, (name, pair) in enumerate(zip(names, pairs)):
+                    codes = live[name + "_codes", step]
+                    scales = live[name + "_scales", step]
+                    for g in range(PASSES):
+                        cols = slice(g * P, (g + 1) * P)
+                        nc.tensor.matmul_mx(
+                            out=product[:, x, :],
+                            lhsT=codes[:, cols].bitcast(FP8X4),
+                            lhsT_scale=scales[:, cols],
+                            rhs=live["value_codes", batch][:, pair, cols].bitcast(FP8X4),
+                            rhs_scale=live["value_scales", batch][:, pair, cols],
+                            start=(y * PASSES + g == 0),
+                            stop=(y * PASSES + g == last),
+                        )
+            live["product", step] = product
+
+        def store(step):
+            batch, i = divmod(step, QUERY_TILES)
+            if i % CHUNK == 0:
+                live["result"] = sb([P, CHUNK, 2, CHANNELS], F32, "result", 2)
+            result = live["result"]
+            nc.vector.tensor_copy(out=result[:, i % CHUNK, :, :], in_=live["product", step][:])
+            if i % CHUNK == CHUNK - 1:
+                rows = out[batch].rearrange("(p i) x e -> p i x e", i=QUERY_TILES)
+                nc.sync.dma_start(out=rows[:, i + 1 - CHUNK : i + 1, :, :], in_=result[:])
+
+        flips = [("keys", 2), ("keys", 3), ("keys", 4), ("queries", 1), ("keys", 0), ("keys", 1), ("queries", 0)]
+
+        def load_flip(batch, job):
+            kind, index = flips[job]
+            if kind == "keys":
+                load_keys(batch, index)
+            elif index == 1:
+                load_queries(batch)
+
+        def flip(batch, job):
+            kind, index = flips[job]
+            if kind == "keys":
+                transpose_keys(batch, index)
+            else:
+                transpose_queries(batch, index)
+
+        for job in range(len(flips)):
+            load_flip(0, job)
+            flip(0, job)
+        for pair in range(N_PAIRS):
+            load_values(0, pair)
+            group_values(0, pair)
+            quantise_values(0, pair)
+
+        def in_range(step):
+            return 0 <= step < STEPS
+
+        for s in range(-SCORES_AHEAD, STEPS + 3):
+            batch, job = divmod(s + LOAD_AHEAD + 3, QUERY_TILES)
+            if job < len(flips) and batch + 1 < BATCHES:
+                load_flip(batch + 1, job)
+            batch, pair = divmod(s + LOAD_AHEAD - 3, QUERY_TILES)
+            if batch >= 0 and pair < N_PAIRS and batch + 1 < BATCHES:
+                load_values(batch + 1, pair)
+
+            if in_range(s - 3):
+                multiply(s - 3)
+            batch, job = divmod(s + 3, QUERY_TILES)
+            if batch >= 0 and job < len(flips) and batch + 1 < BATCHES:
+                flip(batch + 1, job)
+
+            if in_range(s):
+                head2_logit(s)
+            batch, pair = divmod(s - 3, QUERY_TILES)
+            values_due = batch >= 0 and pair < N_PAIRS and batch + 1 < BATCHES
+            if values_due:
+                group_values(batch + 1, pair)
+            if in_range(s + SHARE_AHEAD):
+                head2_share1(s + SHARE_AHEAD)
+            if in_range(s):
+                head2_share2(s)
+                head1_series(s)
+                head2_split(s)
+            if in_range(s - 1):
+                head2_products(s - 1)
+                quantise_series("h1y0", s - 1)
+                quantise_series("h1y1", s - 1)
+            if in_range(s - 2):
+                quantise_series("h2y0", s - 2)
+                quantise_series("h2y1", s - 2)
+                quantise_series("h2y2", s - 2)
+            if values_due:
+                quantise_values(batch + 1, pair)
+            if in_range(s - 3):
+                store(s - 3)
+            if in_range(s + SCORES_AHEAD):
+                head2_differences(s + SCORES_AHEAD)
+            if (s + 1) % CHUNK == 0 and in_range(s + 1):
+                for step in range(s + 1, s + 1 + CHUNK):
+                    head2_log_share1(step)

@@ -214,8 +214,8 @@ def tile_anomalyattention_pa_t_kernel(tc, q_plus, key_plus, retrieval, out):
             rest = live["rest", step]
             y1 = sb([P, STEP], BF16, "h2y1", 2)
             y2 = sb([P, STEP], BF16, "h2y2", 2)
-            nc.gpsimd.tensor_tensor(out=y1[:], in0=rest[:], in1=live["share1", step][:], op=ALU.mult)
-            nc.gpsimd.tensor_tensor(out=y2[:], in0=rest[:], in1=live["share2", step][:], op=ALU.mult)
+            nc.vector.tensor_tensor(out=y1[:], in0=rest[:], in1=live["share1", step][:], op=ALU.mult)
+            nc.vector.tensor_tensor(out=y2[:], in0=rest[:], in1=live["share2", step][:], op=ALU.mult)
             live["h2y1", step] = y1
             live["h2y2", step] = y2
 

@@ -61,7 +61,7 @@ def tile_anomalyattention_pa_t_kernel(tc, q_plus, key_plus, retrieval, out):
         live = {}
 
         def load_keys(batch, pair):
-            raw = sb([P, PASSES, PACK, CHANNELS], BF16, "key_raw", LOAD_AHEAD + 1)
+            raw = sb([P, PASSES, PACK, CHANNELS], BF16, "key_raw", N_PAIRS)
             nc.sync.dma_start(
                 out=raw[:],
                 in_=key_plus[batch, pair].rearrange("(g p t) e -> p g t e", g=PASSES, t=PACK),
@@ -70,12 +70,15 @@ def tile_anomalyattention_pa_t_kernel(tc, q_plus, key_plus, retrieval, out):
 
         def transpose_keys(batch, pair):
             raw = live["key_raw", batch, pair]
-            flipped = psum.tile([P, PASSES, PACK, P], BF16, name="flipped", tag="flipped", bufs=1)
+            flipped = psum.tile([P, PASSES, PACK, P], BF16, name="flipped", tag="flipped", bufs=2)
             for g in range(PASSES):
                 for t in range(PACK):
                     nc.tensor.transpose(out=flipped[:, g, t, :], in_=raw[:, g, t, :], identity=identity[:])
+            live["flipped"] = flipped
+
+        def keep_keys(batch, pair):
             keys_t = sb([P, PASSES, PACK, P], BF16, "keys_t%d" % pair, 2)
-            nc.vector.tensor_copy(out=keys_t[:], in_=flipped[:])
+            nc.vector.tensor_copy(out=keys_t[:], in_=live["flipped"][:])
             live["keys_t", batch, pair] = keys_t
 
         def load_queries(batch):
@@ -87,9 +90,13 @@ def tile_anomalyattention_pa_t_kernel(tc, q_plus, key_plus, retrieval, out):
 
         def transpose_queries(batch, head):
             raw = live["query_raw", batch]
-            flipped = psum.tile([P, QUERY_TILES, P], BF16, name="flipped", tag="flipped", bufs=1)
+            flipped = psum.tile([P, QUERY_TILES, P], BF16, name="flipped", tag="flipped", bufs=2)
             for i in range(QUERY_TILES):
                 nc.tensor.transpose(out=flipped[:, i, :], in_=raw[:, i, head, :], identity=identity[:])
+            live["flipped"] = flipped
+
+        def keep_queries(batch, head):
+            flipped = live["flipped"]
             queries_t = sb([P, QUERY_TILES, P], BF16, "queries_t%d" % head, 2)
             nc.vector.tensor_copy(out=queries_t[:], in_=flipped[:])
             live["queries_t", batch, head] = queries_t
@@ -123,8 +130,8 @@ def tile_anomalyattention_pa_t_kernel(tc, q_plus, key_plus, retrieval, out):
                 in_=grouped[:].rearrange("p g e t -> p (g e t)"),
             )
 
-        def score_bank(tag, batch, i, g, terms):
-            bank = psum.tile([P, PACK, P], F32, name=tag, tag=tag, bufs=3)
+        def score_bank(tag, bufs, i, g, terms):
+            bank = psum.tile([P, PACK, P], F32, name=tag, tag=tag, bufs=bufs)
             for t in range(PACK):
                 for j, (keys_t, queries_t) in enumerate(terms):
                     nc.tensor.matmul(
@@ -136,10 +143,10 @@ def tile_anomalyattention_pa_t_kernel(tc, q_plus, key_plus, retrieval, out):
                     )
             return bank
 
-        def quantise_series(name, step):
+        def quantise_series(name, step, bufs):
             series = live[name, step]
-            codes = sb([P, PASSES * P], U32, name + "_codes", 3)
-            scales = sb([P, PASSES * P], U8, name + "_scales", 3)
+            codes = sb([P, PASSES * P], U32, name + "_codes", bufs)
+            scales = sb([P, PASSES * P], U8, name + "_scales", bufs)
             nc.vector.quantize_mx(out=codes[:].bitcast(FP8X4), scales=scales[:], in_=series[:])
             live[name + "_codes", step] = codes
             live[name + "_scales", step] = scales
@@ -150,7 +157,7 @@ def tile_anomalyattention_pa_t_kernel(tc, q_plus, key_plus, retrieval, out):
             second = sb([P, STEP], BF16, "h1y1", 2)
             for g in range(PASSES):
                 gap = score_bank(
-                    "gap", batch, i, g,
+                    "gap", 2, i, g,
                     [
                         (live["keys_t", batch, 0], live["queries_t", batch, 0]),
                         (live["keys_t", batch, 1], live["minus_queries_t", batch]),
@@ -166,12 +173,16 @@ def tile_anomalyattention_pa_t_kernel(tc, q_plus, key_plus, retrieval, out):
             queries_t = live["queries_t", batch, 1]
             d12 = sb([P, STEP], F32, "d12", SCORES_AHEAD + 1)
             d01 = sb([P, STEP], F32, "d01", SCORES_AHEAD + 1)
+            scaled = []
             for g in range(PASSES):
-                s1 = score_bank("score", batch, i, g, [(live["keys_t", batch, 3], queries_t)])
-                s2 = score_bank("score", batch, i, g, [(live["keys_t", batch, 4], queries_t)])
-                s0 = score_bank("score", batch, i, g, [(live["keys_t", batch, 2], queries_t)])
-                a1 = sb([P, P, PACK], F32, "a1", 2)
+                s1 = score_bank("score", 3, i, g, [(live["keys_t", batch, 3], queries_t)])
+                a1 = sb([P, P, PACK], F32, "a1", PASSES)
                 nc.vector.tensor_scalar_mul(out=a1[:], in0=by_query(s1), scalar1=SCALE)
+                scaled.append(a1)
+            for g in range(PASSES):
+                a1 = scaled[g]
+                s2 = score_bank("score", 3, i, g, [(live["keys_t", batch, 4], queries_t)])
+                s0 = score_bank("score", 3, i, g, [(live["keys_t", batch, 2], queries_t)])
                 nc.vector.scalar_tensor_tensor(
                     out=half(d12, g), in0=by_query(s2), scalar=-SCALE, in1=a1[:], op0=ALU.mult, op1=ALU.add
                 )
@@ -191,20 +202,23 @@ def tile_anomalyattention_pa_t_kernel(tc, q_plus, key_plus, retrieval, out):
             nc.scalar.activation(out=logit[:], in_=live["share1", step][:], func=FUNC.Ln, bias=tiny[:])
             live["logit", step] = logit
 
-        def head2_logit(step):
+        def head2_cap(step):
             logit = live["logit", step]
             nc.vector.tensor_tensor(out=logit[:], in0=live["d12", step][:], in1=logit[:], op=ALU.min)
+
+        def head2_logit(step):
+            logit = live["logit", step]
             nc.vector.tensor_tensor(out=logit[:], in0=live["d01", step][:], in1=logit[:], op=ALU.add)
 
         def head2_share2(step):
-            share2 = sb([P, STEP], F32, "share2", 2)
+            share2 = sb([P, STEP], F32, "share2", 3)
             nc.scalar.activation(out=share2[:], in_=live["d12", step][:], func=FUNC.Sigmoid, scale=-1.0)
             live["share2", step] = share2
 
         def head2_split(step):
             logit = live["logit", step]
             y0 = sb([P, STEP], BF16, "h2y0", 3)
-            rest = sb([P, STEP], F32, "rest", 2)
+            rest = sb([P, STEP], F32, "rest", 3)
             nc.scalar.activation(out=y0[:], in_=logit[:], func=FUNC.Sigmoid)
             nc.scalar.activation(out=rest[:], in_=logit[:], func=FUNC.Sigmoid, scale=-1.0)
             live["h2y0", step] = y0
@@ -214,8 +228,10 @@ def tile_anomalyattention_pa_t_kernel(tc, q_plus, key_plus, retrieval, out):
             rest = live["rest", step]
             y1 = sb([P, STEP], BF16, "h2y1", 2)
             y2 = sb([P, STEP], BF16, "h2y2", 2)
-            nc.vector.tensor_tensor(out=y1[:], in0=rest[:], in1=live["share1", step][:], op=ALU.mult)
-            nc.vector.tensor_tensor(out=y2[:], in0=rest[:], in1=live["share2", step][:], op=ALU.mult)
+            for share, series in ((live["share1", step], y1), (live["share2", step], y2)):
+                for g in range(PASSES):
+                    cols = slice(g * BANK, (g + 1) * BANK)
+                    nc.gpsimd.tensor_tensor(out=series[:, cols], in0=rest[:, cols], in1=share[:, cols], op=ALU.mult)
             live["h2y1", step] = y1
             live["h2y2", step] = y2
 
@@ -270,53 +286,66 @@ def tile_anomalyattention_pa_t_kernel(tc, q_plus, key_plus, retrieval, out):
             else:
                 transpose_queries(batch, index)
 
-        for job in range(len(flips)):
-            load_flip(0, job)
-            flip(0, job)
-        for pair in range(N_PAIRS):
-            load_values(0, pair)
-            group_values(0, pair)
-            quantise_values(0, pair)
+        def keep_flip(batch, job):
+            kind, index = flips[job]
+            if kind == "keys":
+                keep_keys(batch, index)
+            else:
+                keep_queries(batch, index)
 
         def in_range(step):
             return 0 <= step < STEPS
 
-        for s in range(-SCORES_AHEAD, STEPS + 3):
-            batch, job = divmod(s + LOAD_AHEAD + 3, QUERY_TILES)
-            if job < len(flips) and batch + 1 < BATCHES:
-                load_flip(batch + 1, job)
-            batch, pair = divmod(s + LOAD_AHEAD - 3, QUERY_TILES)
-            if batch >= 0 and pair < N_PAIRS and batch + 1 < BATCHES:
-                load_values(batch + 1, pair)
+        def due(step, jobs):
+            batch, job = divmod(step, QUERY_TILES)
+            return 0 <= batch + 1 < BATCHES and job < jobs, batch + 1, job
+
+        first_flip = -QUERY_TILES - 1
+        for s in range(first_flip - LOAD_AHEAD, STEPS + 3):
+            load_due, batch, job = due(s + LOAD_AHEAD + 1, len(flips))
+            if load_due:
+                load_flip(batch, job)
+            load_due, batch, pair = due(s + LOAD_AHEAD - 6, N_PAIRS)
+            if load_due:
+                load_values(batch, pair)
+            flip_due, flip_batch, job = due(s + 1, len(flips))
+            values_due, values_batch, pair = due(s - 6, N_PAIRS)
 
             if in_range(s - 3):
                 multiply(s - 3)
-            batch, job = divmod(s + 3, QUERY_TILES)
-            if batch >= 0 and job < len(flips) and batch + 1 < BATCHES:
-                flip(batch + 1, job)
+            if flip_due:
+                flip(flip_batch, job)
 
             if in_range(s):
+                head2_cap(s)
+            if in_range(s - 1):
+                quantise_series("h1y0", s - 1, 3)
+            if in_range(s):
                 head2_logit(s)
-            batch, pair = divmod(s - 3, QUERY_TILES)
-            values_due = batch >= 0 and pair < N_PAIRS and batch + 1 < BATCHES
+            if in_range(s - 1):
+                quantise_series("h1y1", s - 1, 3)
             if values_due:
-                group_values(batch + 1, pair)
+                group_values(values_batch, pair)
+            if in_range(s - 2):
+                quantise_series("h2y0", s - 2, 2)
+                quantise_series("h2y1", s - 2, 2)
+                quantise_series("h2y2", s - 2, 2)
+            if values_due:
+                quantise_values(values_batch, pair)
+
             if in_range(s + SHARE_AHEAD):
                 head2_share1(s + SHARE_AHEAD)
             if in_range(s):
                 head2_share2(s)
+            if in_range(s):
                 head1_series(s)
+            if in_range(s):
                 head2_split(s)
             if in_range(s - 1):
                 head2_products(s - 1)
-                quantise_series("h1y0", s - 1)
-                quantise_series("h1y1", s - 1)
-            if in_range(s - 2):
-                quantise_series("h2y0", s - 2)
-                quantise_series("h2y1", s - 2)
-                quantise_series("h2y2", s - 2)
-            if values_due:
-                quantise_values(batch + 1, pair)
+
+            if flip_due:
+                keep_flip(flip_batch, job)
             if in_range(s - 3):
                 store(s - 3)
             if in_range(s + SCORES_AHEAD):

@@ -228,10 +228,9 @@ def tile_anomalyattention_pa_t_kernel(tc, q_plus, key_plus, retrieval, out):
             rest = live["rest", step]
             y1 = sb([P, STEP], BF16, "h2y1", 2)
             y2 = sb([P, STEP], BF16, "h2y2", 2)
-            for share, series in ((live["share1", step], y1), (live["share2", step], y2)):
-                for g in range(PASSES):
-                    cols = slice(g * BANK, (g + 1) * BANK)
-                    nc.gpsimd.tensor_tensor(out=series[:, cols], in0=rest[:, cols], in1=share[:, cols], op=ALU.mult)
+            engine = nc.gpsimd if in_range(step + 1 + SCORES_AHEAD) else nc.vector
+            engine.tensor_tensor(out=y1[:], in0=rest[:], in1=live["share1", step][:], op=ALU.mult)
+            engine.tensor_tensor(out=y2[:], in0=rest[:], in1=live["share2", step][:], op=ALU.mult)
             live["h2y1", step] = y1
             live["h2y2", step] = y2
 

@@ -18,6 +18,7 @@ CHANNELS = 128
 N_PAIRS = 5
 HEAD1_PAIRS = (0, 1)
 HEAD2_PAIRS = (2, 3, 4)
+NEGATED_PAIRS = (1, 3)
 SCALE = 1.0 / math.sqrt(CHANNELS)
 
 P = 128
@@ -70,7 +71,7 @@ def tile_anomalyattention_pa_t_kernel(tc, q_plus, key_plus, retrieval, out):
 
         def transpose_keys(batch, pair):
             raw = live["key_raw", batch, pair]
-            flipped = psum.tile([P, PASSES, PACK, P], BF16, name="flipped", tag="flipped", bufs=2)
+            flipped = psum.tile([P, PASSES, PACK, P], BF16, name="flipped", tag="flipped", bufs=1)
             for g in range(PASSES):
                 for t in range(PACK):
                     nc.tensor.transpose(out=flipped[:, g, t, :], in_=raw[:, g, t, :], identity=identity[:])
@@ -78,7 +79,10 @@ def tile_anomalyattention_pa_t_kernel(tc, q_plus, key_plus, retrieval, out):
 
         def keep_keys(batch, pair):
             keys_t = sb([P, PASSES, PACK, P], BF16, "keys_t%d" % pair, 2)
-            nc.vector.tensor_copy(out=keys_t[:], in_=live["flipped"][:])
+            if pair in NEGATED_PAIRS:
+                nc.vector.tensor_scalar_mul(out=keys_t[:], in0=live["flipped"][:], scalar1=-1.0)
+            else:
+                nc.vector.tensor_copy(out=keys_t[:], in_=live["flipped"][:])
             live["keys_t", batch, pair] = keys_t
 
         def load_queries(batch):
@@ -90,7 +94,7 @@ def tile_anomalyattention_pa_t_kernel(tc, q_plus, key_plus, retrieval, out):
 
         def transpose_queries(batch, head):
             raw = live["query_raw", batch]
-            flipped = psum.tile([P, QUERY_TILES, P], BF16, name="flipped", tag="flipped", bufs=2)
+            flipped = psum.tile([P, QUERY_TILES, P], BF16, name="flipped", tag="flipped", bufs=1)
             for i in range(QUERY_TILES):
                 nc.tensor.transpose(out=flipped[:, i, :], in_=raw[:, i, head, :], identity=identity[:])
             live["flipped"] = flipped
@@ -100,10 +104,6 @@ def tile_anomalyattention_pa_t_kernel(tc, q_plus, key_plus, retrieval, out):
             queries_t = sb([P, QUERY_TILES, P], BF16, "queries_t%d" % head, 2)
             nc.vector.tensor_copy(out=queries_t[:], in_=flipped[:])
             live["queries_t", batch, head] = queries_t
-            if head == 0:
-                minus_t = sb([P, QUERY_TILES, P], BF16, "minus_queries_t", 2)
-                nc.vector.tensor_scalar_mul(out=minus_t[:], in0=flipped[:], scalar1=-1.0)
-                live["minus_queries_t", batch] = minus_t
 
         def load_values(batch, pair):
             raw = sb([P, PASSES, PACK, CHANNELS], BF16, "value_raw", LOAD_AHEAD + 1)
@@ -130,16 +130,17 @@ def tile_anomalyattention_pa_t_kernel(tc, q_plus, key_plus, retrieval, out):
                 in_=grouped[:].rearrange("p g e t -> p (g e t)"),
             )
 
-        def score_bank(tag, bufs, i, g, terms):
+        def score_bank(tag, bufs, step, head, g, pairs):
+            batch, i = divmod(step, QUERY_TILES)
             bank = psum.tile([P, PACK, P], F32, name=tag, tag=tag, bufs=bufs)
             for t in range(PACK):
-                for j, (keys_t, queries_t) in enumerate(terms):
+                for j, pair in enumerate(pairs):
                     nc.tensor.matmul(
                         out=bank[:, t, :],
-                        lhsT=keys_t[:, g, t, :],
-                        rhs=queries_t[:, i, :],
+                        lhsT=live["keys_t", batch, pair][:, g, t, :],
+                        rhs=live["queries_t", batch, head][:, i, :],
                         start=(j == 0),
-                        stop=(j == len(terms) - 1),
+                        stop=(j == len(pairs) - 1),
                     )
             return bank
 
@@ -152,45 +153,36 @@ def tile_anomalyattention_pa_t_kernel(tc, q_plus, key_plus, retrieval, out):
             live[name + "_scales", step] = scales
 
         def head1_series(step):
-            batch, i = divmod(step, QUERY_TILES)
             first = sb([P, STEP], BF16, "h1y0", 2)
             second = sb([P, STEP], BF16, "h1y1", 2)
             for g in range(PASSES):
-                gap = score_bank(
-                    "gap", 2, i, g,
-                    [
-                        (live["keys_t", batch, 0], live["queries_t", batch, 0]),
-                        (live["keys_t", batch, 1], live["minus_queries_t", batch]),
-                    ],
-                )
+                gap = score_bank("gap", 2, step, 0, g, (0, 1))
                 nc.scalar.activation(out=half(first, g), in_=by_query(gap), func=FUNC.Sigmoid, scale=SCALE)
                 nc.scalar.activation(out=half(second, g), in_=by_query(gap), func=FUNC.Sigmoid, scale=-SCALE)
             live["h1y0", step] = first
             live["h1y1", step] = second
 
         def head2_differences(step):
-            batch, i = divmod(step, QUERY_TILES)
-            queries_t = live["queries_t", batch, 1]
             d12 = sb([P, STEP], F32, "d12", SCORES_AHEAD + 1)
-            d01 = sb([P, STEP], F32, "d01", SCORES_AHEAD + 1)
-            scaled = []
-            for g in range(PASSES):
-                s1 = score_bank("score", 3, i, g, [(live["keys_t", batch, 3], queries_t)])
-                a1 = sb([P, P, PACK], F32, "a1", PASSES)
-                nc.vector.tensor_scalar_mul(out=a1[:], in0=by_query(s1), scalar1=SCALE)
-                scaled.append(a1)
-            for g in range(PASSES):
-                a1 = scaled[g]
-                s2 = score_bank("score", 3, i, g, [(live["keys_t", batch, 4], queries_t)])
-                s0 = score_bank("score", 3, i, g, [(live["keys_t", batch, 2], queries_t)])
-                nc.vector.scalar_tensor_tensor(
-                    out=half(d12, g), in0=by_query(s2), scalar=-SCALE, in1=a1[:], op0=ALU.mult, op1=ALU.add
-                )
-                nc.vector.scalar_tensor_tensor(
-                    out=half(d01, g), in0=by_query(s0), scalar=SCALE, in1=a1[:], op0=ALU.mult, op1=ALU.subtract
-                )
+            d01 = sb([P, BANK], F32, "d01", SCORES_AHEAD + 1)
+            s21 = score_bank("score", 4, step, 1, 0, (3, 4))
+            nc.vector.tensor_scalar_mul(out=half(d12, 0), in0=by_query(s21), scalar1=-SCALE)
+            minus_s1 = score_bank("score", 4, step, 1, 1, (3,))
+            a1 = sb([P, P, PACK], F32, "a1", 2)
+            nc.vector.tensor_scalar_mul(out=a1[:], in0=by_query(minus_s1), scalar1=-SCALE)
+            s2 = score_bank("score", 4, step, 1, 1, (4,))
+            s0 = score_bank("score", 4, step, 1, 1, (2,))
+            nc.vector.scalar_tensor_tensor(
+                out=half(d12, 1), in0=by_query(s2), scalar=-SCALE, in1=a1[:], op0=ALU.mult, op1=ALU.add
+            )
+            nc.vector.scalar_tensor_tensor(
+                out=half(d01, 0), in0=by_query(s0), scalar=SCALE, in1=a1[:], op0=ALU.mult, op1=ALU.subtract
+            )
             live["d12", step] = d12
             live["d01", step] = d01
+
+        def head2_late_difference(step):
+            live["s01", step] = score_bank("score", 4, step, 1, 0, (2, 3))
 
         def head2_share1(step):
             share1 = sb([P, STEP], F32, "share1", SHARE_AHEAD + 2)
@@ -206,9 +198,16 @@ def tile_anomalyattention_pa_t_kernel(tc, q_plus, key_plus, retrieval, out):
             logit = live["logit", step]
             nc.vector.tensor_tensor(out=logit[:], in0=live["d12", step][:], in1=logit[:], op=ALU.min)
 
-        def head2_logit(step):
+        def head2_logit_pass0(step):
             logit = live["logit", step]
-            nc.vector.tensor_tensor(out=logit[:], in0=live["d01", step][:], in1=logit[:], op=ALU.add)
+            nc.vector.scalar_tensor_tensor(
+                out=half(logit, 0), in0=by_query(live["s01", step]), scalar=SCALE, in1=half(logit, 0),
+                op0=ALU.mult, op1=ALU.add,
+            )
+
+        def head2_logit_pass1(step):
+            logit = live["logit", step]
+            nc.vector.tensor_tensor(out=half(logit, 1), in0=half(live["d01", step], 0), in1=half(logit, 1), op=ALU.add)
 
         def head2_share2(step):
             share2 = sb([P, STEP], F32, "share2", 3)
@@ -314,15 +313,19 @@ def tile_anomalyattention_pa_t_kernel(tc, q_plus, key_plus, retrieval, out):
                 multiply(s - 3)
             if flip_due:
                 flip(flip_batch, job)
+            if in_range(s):
+                head2_late_difference(s)
 
             if in_range(s):
                 head2_cap(s)
             if in_range(s - 1):
                 quantise_series("h1y0", s - 1, 3)
             if in_range(s):
-                head2_logit(s)
+                head2_logit_pass1(s)
             if in_range(s - 1):
                 quantise_series("h1y1", s - 1, 3)
+            if in_range(s):
+                head2_logit_pass0(s)
             if values_due:
                 group_values(values_batch, pair)
             if in_range(s - 2):

@@ -223,15 +223,12 @@ def tile_anomalyattention_pa_t_kernel(tc, q_plus, key_plus, retrieval, out):
             live["h2y0", step] = y0
             live["rest", step] = rest
 
-        def head2_products(step):
-            rest = live["rest", step]
-            y1 = sb([P, STEP], BF16, "h2y1", 2)
-            y2 = sb([P, STEP], BF16, "h2y2", 2)
-            engine = nc.gpsimd if in_range(step + 1 + SCORES_AHEAD) else nc.vector
-            engine.tensor_tensor(out=y1[:], in0=rest[:], in1=live["share1", step][:], op=ALU.mult)
-            engine.tensor_tensor(out=y2[:], in0=rest[:], in1=live["share2", step][:], op=ALU.mult)
-            live["h2y1", step] = y1
-            live["h2y2", step] = y2
+        def head2_product(step, engine, y):
+            product = sb([P, STEP], BF16, "h2y%d" % y, 2)
+            engine.tensor_tensor(
+                out=product[:], in0=live["rest", step][:], in1=live["share%d" % y, step][:], op=ALU.mult
+            )
+            live["h2y%d" % y, step] = product
 
         def multiply(step):
             batch = step // QUERY_TILES
@@ -334,6 +331,8 @@ def tile_anomalyattention_pa_t_kernel(tc, q_plus, key_plus, retrieval, out):
                 quantise_series("h2y2", s - 2, 2)
             if values_due:
                 quantise_values(values_batch, pair)
+            if in_range(s - 1):
+                head2_product(s - 1, nc.vector, 2)
 
             if in_range(s + SHARE_AHEAD):
                 head2_share1(s + SHARE_AHEAD)
@@ -344,7 +343,7 @@ def tile_anomalyattention_pa_t_kernel(tc, q_plus, key_plus, retrieval, out):
             if in_range(s):
                 head2_split(s)
             if in_range(s - 1):
-                head2_products(s - 1)
+                head2_product(s - 1, nc.gpsimd, 1)
 
             if flip_due:
                 keep_flip(flip_batch, job)

@@ -18,6 +18,7 @@ CHANNELS = 128
 N_PAIRS = 5
 HEAD1_PAIRS = (0, 1)
 HEAD2_PAIRS = (2, 3, 4)
+LATE_PAIRS = (2, 3)
 NEGATED_PAIRS = (1, 3)
 SCALE = 1.0 / math.sqrt(CHANNELS)
 
@@ -28,9 +29,14 @@ QUERY_TILES = LENGTH // P
 BANK = P * PACK
 STEP = PASSES * BANK
 STEPS = BATCHES * QUERY_TILES
-CHUNK = 4
-SCORES_AHEAD = 5
-SHARE_AHEAD = 4
+CHUNKS = (2, 4, 4, 4, 4, 4, 4, 4, 2)
+CHUNK_BUFS = max(CHUNKS) + 2
+HEAD1_AHEAD = 4
+STORE_STEPS = 2
+FLIP_AHEAD = 13
+VALUE_AT = (-HEAD1_AHEAD, 1 - HEAD1_AHEAD, 1, 2, 3)
+BANKS = 5
+SPLIT_LAG = 1
 LOAD_AHEAD = 2
 TINY = 2.0**-60
 
@@ -62,7 +68,7 @@ def tile_anomalyattention_pa_t_kernel(tc, q_plus, key_plus, retrieval, out):
         live = {}
 
         def load_keys(batch, pair):
-            raw = sb([P, PASSES, PACK, CHANNELS], BF16, "key_raw", N_PAIRS)
+            raw = sb([P, PASSES, PACK, CHANNELS], BF16, "key_raw", 5)
             nc.sync.dma_start(
                 out=raw[:],
                 in_=key_plus[batch, pair].rearrange("(g p t) e -> p g t e", g=PASSES, t=PACK),
@@ -71,18 +77,19 @@ def tile_anomalyattention_pa_t_kernel(tc, q_plus, key_plus, retrieval, out):
 
         def transpose_keys(batch, pair):
             raw = live["key_raw", batch, pair]
-            flipped = psum.tile([P, PASSES, PACK, P], BF16, name="flipped", tag="flipped", bufs=1)
+            flipped = psum.tile([P, PASSES, PACK, P], BF16, name="bank", tag="bank", bufs=BANKS)
             for g in range(PASSES):
                 for t in range(PACK):
                     nc.tensor.transpose(out=flipped[:, g, t, :], in_=raw[:, g, t, :], identity=identity[:])
-            live["flipped"] = flipped
+            live["flipped_keys", batch, pair] = flipped
 
         def keep_keys(batch, pair):
-            keys_t = sb([P, PASSES, PACK, P], BF16, "keys_t%d" % pair, 2)
+            flipped = live["flipped_keys", batch, pair]
+            keys_t = sb([P, PASSES, PACK, P], BF16, "keys_t%d" % pair, 3 if pair in LATE_PAIRS else 2)
             if pair in NEGATED_PAIRS:
-                nc.vector.tensor_scalar_mul(out=keys_t[:], in0=live["flipped"][:], scalar1=-1.0)
+                nc.vector.tensor_scalar_mul(out=keys_t[:], in0=flipped[:], scalar1=-1.0)
             else:
-                nc.vector.tensor_copy(out=keys_t[:], in_=live["flipped"][:])
+                nc.vector.tensor_copy(out=keys_t[:], in_=flipped[:])
             live["keys_t", batch, pair] = keys_t
 
         def load_queries(batch):
@@ -94,19 +101,19 @@ def tile_anomalyattention_pa_t_kernel(tc, q_plus, key_plus, retrieval, out):
 
         def transpose_queries(batch, head):
             raw = live["query_raw", batch]
-            flipped = psum.tile([P, QUERY_TILES, P], BF16, name="flipped", tag="flipped", bufs=1)
+            flipped = psum.tile([P, QUERY_TILES, P], BF16, name="bank", tag="bank", bufs=BANKS)
             for i in range(QUERY_TILES):
                 nc.tensor.transpose(out=flipped[:, i, :], in_=raw[:, i, head, :], identity=identity[:])
-            live["flipped"] = flipped
+            live["flipped_queries", batch, head] = flipped
 
         def keep_queries(batch, head):
-            flipped = live["flipped"]
-            queries_t = sb([P, QUERY_TILES, P], BF16, "queries_t%d" % head, 2)
+            flipped = live["flipped_queries", batch, head]
+            queries_t = sb([P, QUERY_TILES, P], BF16, "queries_t%d" % head, 2 + head)
             nc.vector.tensor_copy(out=queries_t[:], in_=flipped[:])
             live["queries_t", batch, head] = queries_t
 
         def load_values(batch, pair):
-            raw = sb([P, PASSES, PACK, CHANNELS], BF16, "value_raw", LOAD_AHEAD + 1)
+            raw = sb([P, PASSES, PACK, CHANNELS], BF16, "value_raw", 2)
             nc.sync.dma_start(
                 out=raw[:],
                 in_=retrieval[batch, pair].rearrange("(g p t) e -> p g t e", g=PASSES, t=PACK),
@@ -116,17 +123,21 @@ def tile_anomalyattention_pa_t_kernel(tc, q_plus, key_plus, retrieval, out):
         def group_values(batch, pair):
             raw = live["value_raw", batch, pair]
             grouped = sb([P, PASSES, CHANNELS, PACK], BF16, "value_grouped", 2)
-            nc.vector.tensor_copy(out=grouped[:], in_=raw[:].rearrange("p g t e -> p g e t"))
+            nc.gpsimd.tensor_scalar(
+                out=grouped[:], in0=raw[:].rearrange("p g t e -> p g e t"), scalar1=1.0, scalar2=0.0,
+                op0=ALU.mult, op1=ALU.add,
+            )
             live["value_grouped", batch, pair] = grouped
 
         def quantise_values(batch, pair):
             grouped = live["value_grouped", batch, pair]
-            if pair == 0:
-                live["value_codes", batch] = sb([P, N_PAIRS, PASSES * CHANNELS], U32, "value_codes", 2)
-                live["value_scales", batch] = sb([P, N_PAIRS, PASSES * CHANNELS], U8, "value_scales", 2)
+            codes = sb([P, PASSES * CHANNELS], U32, "value_codes%d" % pair, 2)
+            scales = sb([P, PASSES * CHANNELS], U8, "value_scales%d" % pair, 2)
+            live["value_codes", batch, pair] = codes
+            live["value_scales", batch, pair] = scales
             nc.vector.quantize_mx(
-                out=live["value_codes", batch][:, pair, :].bitcast(FP8X4),
-                scales=live["value_scales", batch][:, pair, :],
+                out=codes[:].bitcast(FP8X4),
+                scales=scales[:],
                 in_=grouped[:].rearrange("p g e t -> p (g e t)"),
             )
 
@@ -144,34 +155,34 @@ def tile_anomalyattention_pa_t_kernel(tc, q_plus, key_plus, retrieval, out):
                     )
             return bank
 
-        def quantise_series(name, step, bufs):
+        def quantise_series(name, count, step, bufs):
             series = live[name, step]
-            codes = sb([P, PASSES * P], U32, name + "_codes", bufs)
-            scales = sb([P, PASSES * P], U8, name + "_scales", bufs)
+            codes = sb([P, count * PASSES * P], U32, name + "_codes", bufs)
+            scales = sb([P, count * PASSES * P], U8, name + "_scales", bufs)
             nc.vector.quantize_mx(out=codes[:].bitcast(FP8X4), scales=scales[:], in_=series[:])
             live[name + "_codes", step] = codes
             live[name + "_scales", step] = scales
 
         def head1_series(step):
-            first = sb([P, STEP], BF16, "h1y0", 2)
-            second = sb([P, STEP], BF16, "h1y1", 2)
+            both = sb([P, 2 * STEP], BF16, "h1", 2)
+            first = both[:, :STEP]
+            second = both[:, STEP:]
             for g in range(PASSES):
                 gap = score_bank("gap", 2, step, 0, g, (0, 1))
                 nc.scalar.activation(out=half(first, g), in_=by_query(gap), func=FUNC.Sigmoid, scale=SCALE)
                 nc.scalar.activation(out=half(second, g), in_=by_query(gap), func=FUNC.Sigmoid, scale=-SCALE)
-            live["h1y0", step] = first
-            live["h1y1", step] = second
+            live["h1", step] = both
 
         def head2_differences(step):
-            d12 = sb([P, STEP], F32, "d12", SCORES_AHEAD + 1)
-            d01 = sb([P, BANK], F32, "d01", SCORES_AHEAD + 1)
-            s21 = score_bank("score", 4, step, 1, 0, (3, 4))
+            d12 = sb([P, STEP], F32, "d12", CHUNK_BUFS + SPLIT_LAG)
+            d01 = sb([P, BANK], F32, "d01", CHUNK_BUFS)
+            s21 = score_bank("bank", BANKS, step, 1, 0, (3, 4))
             nc.vector.tensor_scalar_mul(out=half(d12, 0), in0=by_query(s21), scalar1=-SCALE)
-            minus_s1 = score_bank("score", 4, step, 1, 1, (3,))
+            minus_s1 = score_bank("bank", BANKS, step, 1, 1, (3,))
             a1 = sb([P, P, PACK], F32, "a1", 2)
             nc.vector.tensor_scalar_mul(out=a1[:], in0=by_query(minus_s1), scalar1=-SCALE)
-            s2 = score_bank("score", 4, step, 1, 1, (4,))
-            s0 = score_bank("score", 4, step, 1, 1, (2,))
+            s2 = score_bank("bank", BANKS, step, 1, 1, (4,))
+            s0 = score_bank("bank", BANKS, step, 1, 1, (2,))
             nc.vector.scalar_tensor_tensor(
                 out=half(d12, 1), in0=by_query(s2), scalar=-SCALE, in1=a1[:], op0=ALU.mult, op1=ALU.add
             )
@@ -182,15 +193,15 @@ def tile_anomalyattention_pa_t_kernel(tc, q_plus, key_plus, retrieval, out):
             live["d01", step] = d01
 
         def head2_late_difference(step):
-            live["s01", step] = score_bank("score", 4, step, 1, 0, (2, 3))
+            live["s01", step] = score_bank("bank", BANKS, step, 1, 0, (2, 3))
 
         def head2_share1(step):
-            share1 = sb([P, STEP], F32, "share1", SHARE_AHEAD + 2)
+            share1 = sb([P, STEP], F32, "share1", CHUNK_BUFS + SPLIT_LAG)
             nc.scalar.activation(out=share1[:], in_=live["d12", step][:], func=FUNC.Sigmoid)
             live["share1", step] = share1
 
         def head2_log_share1(step):
-            logit = sb([P, STEP], F32, "logit", CHUNK)
+            logit = sb([P, STEP], F32, "logit", max(CHUNKS) + SPLIT_LAG)
             nc.scalar.activation(out=logit[:], in_=live["share1", step][:], func=FUNC.Ln, bias=tiny[:])
             live["logit", step] = logit
 
@@ -216,62 +227,80 @@ def tile_anomalyattention_pa_t_kernel(tc, q_plus, key_plus, retrieval, out):
 
         def head2_split(step):
             logit = live["logit", step]
-            y0 = sb([P, STEP], BF16, "h2y0", 3)
+            y02 = sb([P, 2 * STEP], BF16, "h2y02", 3)
+            y0 = y02[:, :STEP]
             rest = sb([P, STEP], F32, "rest", 3)
-            nc.scalar.activation(out=y0[:], in_=logit[:], func=FUNC.Sigmoid)
+            nc.scalar.activation(out=y0, in_=logit[:], func=FUNC.Sigmoid)
             nc.scalar.activation(out=rest[:], in_=logit[:], func=FUNC.Sigmoid, scale=-1.0)
-            live["h2y0", step] = y0
+            live["h2y02", step] = y02
             live["rest", step] = rest
 
         def head2_product(step, engine, y):
-            product = sb([P, STEP], BF16, "h2y%d" % y, 2)
+            if y == 1:
+                tile = sb([P, STEP], BF16, "h2y1", 1)
+                live["h2y1", step] = tile
+                product = tile[:]
+            else:
+                product = live["h2y02", step][:, STEP:]
             engine.tensor_tensor(
-                out=product[:], in0=live["rest", step][:], in1=live["share%d" % y, step][:], op=ALU.mult
+                out=product, in0=live["rest", step][:], in1=live["share%d" % y, step][:], op=ALU.mult
             )
-            live["h2y%d" % y, step] = product
 
-        def multiply(step):
-            batch = step // QUERY_TILES
+        heads = (
+            ((("h1", 0), ("h1", 1)), HEAD1_PAIRS),
+            ((("h2y02", 0), ("h2y1", 0), ("h2y02", 1)), HEAD2_PAIRS),
+        )
+
+        def multiply(steps):
+            if not any(in_range(step) for step in steps):
+                return
             product = psum.tile([P, 2, CHANNELS], F32, name="product", tag="product", bufs=1)
-            heads = (
-                (("h1y0", "h1y1"), HEAD1_PAIRS),
-                (("h2y0", "h2y1", "h2y2"), HEAD2_PAIRS),
-            )
             for x, (names, pairs) in enumerate(heads):
+                step = steps[x]
+                if not in_range(step):
+                    continue
+                batch = step // QUERY_TILES
                 last = len(names) * PASSES - 1
-                for y, (name, pair) in enumerate(zip(names, pairs)):
+                for y, ((name, place), pair) in enumerate(zip(names, pairs)):
                     codes = live[name + "_codes", step]
                     scales = live[name + "_scales", step]
                     for g in range(PASSES):
                         cols = slice(g * P, (g + 1) * P)
+                        series_cols = slice((place * PASSES + g) * P, (place * PASSES + g + 1) * P)
                         nc.tensor.matmul_mx(
                             out=product[:, x, :],
-                            lhsT=codes[:, cols].bitcast(FP8X4),
-                            lhsT_scale=scales[:, cols],
-                            rhs=live["value_codes", batch][:, pair, cols].bitcast(FP8X4),
-                            rhs_scale=live["value_scales", batch][:, pair, cols],
+                            lhsT=codes[:, series_cols].bitcast(FP8X4),
+                            lhsT_scale=scales[:, series_cols],
+                            rhs=live["value_codes", batch, pair][:, cols].bitcast(FP8X4),
+                            rhs_scale=live["value_scales", batch, pair][:, cols],
                             start=(y * PASSES + g == 0),
                             stop=(y * PASSES + g == last),
                         )
-            live["product", step] = product
+            live["product"] = product
 
-        def store(step):
-            batch, i = divmod(step, QUERY_TILES)
-            if i % CHUNK == 0:
-                live["result"] = sb([P, CHUNK, 2, CHANNELS], F32, "result", 2)
+        def store(steps):
+            made = [x for x in range(2) if in_range(steps[x])]
+            if not made:
+                return
+            slot = steps[0] % STORE_STEPS
+            if slot == 0:
+                live["result"] = sb([P, 2, STORE_STEPS, CHANNELS], F32, "result", 2)
             result = live["result"]
-            nc.vector.tensor_copy(out=result[:, i % CHUNK, :, :], in_=live["product", step][:])
-            if i % CHUNK == CHUNK - 1:
-                rows = out[batch].rearrange("(p i) x e -> p i x e", i=QUERY_TILES)
-                nc.sync.dma_start(out=rows[:, i + 1 - CHUNK : i + 1, :, :], in_=result[:])
+            xs = slice(made[0], made[-1] + 1)
+            nc.vector.tensor_copy(out=result[:, xs, slot, :], in_=live["product"][:, xs, :])
+            if slot == STORE_STEPS - 1:
+                for x in made:
+                    batch, i = divmod(steps[x], QUERY_TILES)
+                    rows = out[batch].rearrange("(p i) x e -> p i x e", i=QUERY_TILES)
+                    nc.sync.dma_start(out=rows[:, i + 1 - STORE_STEPS : i + 1, x, :], in_=result[:, x, :, :])
 
-        flips = [("keys", 2), ("keys", 3), ("keys", 4), ("queries", 1), ("keys", 0), ("keys", 1), ("queries", 0)]
+        flips = [("keys", 0), ("keys", 1), ("queries", 0), ("keys", 3), ("keys", 4), ("queries", 1), ("keys", 2)]
 
         def load_flip(batch, job):
             kind, index = flips[job]
             if kind == "keys":
                 load_keys(batch, index)
-            elif index == 1:
+            elif ("query_raw", batch) not in live:
                 load_queries(batch)
 
         def flip(batch, job):
@@ -291,66 +320,75 @@ def tile_anomalyattention_pa_t_kernel(tc, q_plus, key_plus, retrieval, out):
         def in_range(step):
             return 0 <= step < STEPS
 
-        def due(step, jobs):
-            batch, job = divmod(step, QUERY_TILES)
-            return 0 <= batch + 1 < BATCHES and job < jobs, batch + 1, job
+        chunk_starts = [sum(CHUNKS[:n]) for n in range(len(CHUNKS))]
+        share_steps = {}
+        for n, size in enumerate(CHUNKS):
+            before = CHUNKS[max(n - 1, 0)]
+            for j in range(size):
+                share_steps.setdefault(chunk_starts[n] - before + j * before // size, []).append(chunk_starts[n] + j)
 
-        first_flip = -QUERY_TILES - 1
-        for s in range(first_flip - LOAD_AHEAD, STEPS + 3):
-            load_due, batch, job = due(s + LOAD_AHEAD + 1, len(flips))
-            if load_due:
-                load_flip(batch, job)
-            load_due, batch, pair = due(s + LOAD_AHEAD - 6, N_PAIRS)
-            if load_due:
-                load_values(batch, pair)
-            flip_due, flip_batch, job = due(s + 1, len(flips))
-            values_due, values_batch, pair = due(s - 6, N_PAIRS)
+        flip_at = {}
+        for batch in range(BATCHES):
+            for job in range(len(flips)):
+                if batch == 0:
+                    at = -HEAD1_AHEAD - 2 if job < 3 else -HEAD1_AHEAD
+                else:
+                    at = QUERY_TILES * batch - FLIP_AHEAD + (job - 3) % len(flips)
+                flip_at.setdefault(at, []).append((batch, job))
+        value_at = {}
+        for batch in range(BATCHES):
+            for pair in range(N_PAIRS):
+                value_at.setdefault(QUERY_TILES * batch + VALUE_AT[pair], []).append((batch, pair))
 
-            if in_range(s - 3):
-                multiply(s - 3)
-            if flip_due:
-                flip(flip_batch, job)
-            if in_range(s):
-                head2_late_difference(s)
+        last_scores = max(share_steps)
+        for s in range(-HEAD1_AHEAD - 2 - LOAD_AHEAD, STEPS + 4 + SPLIT_LAG):
+            h1 = s + HEAD1_AHEAD
+            h2 = s - SPLIT_LAG
+            multiply((h1 - 2, h2 - 3))
 
             if in_range(s):
                 head2_cap(s)
-            if in_range(s - 1):
-                quantise_series("h1y0", s - 1, 3)
+            if in_range(h1 - 1):
+                quantise_series("h1", 2, h1 - 1, 2)
             if in_range(s):
                 head2_logit_pass1(s)
-            if in_range(s - 1):
-                quantise_series("h1y1", s - 1, 3)
+            if in_range(h2 - 2):
+                quantise_series("h2y02", 2, h2 - 2, 2)
+            for batch, pair in value_at.get(s, ()):
+                quantise_values(batch, pair)
+            if in_range(h2 - 1):
+                head2_product(h2 - 1, nc.vector, 2)
+            if in_range(h2 - 2):
+                quantise_series("h2y1", 1, h2 - 2, 2)
+
+            for step in share_steps.get(s, ()):
+                head2_share1(step)
+            if in_range(h2):
+                head2_share2(h2)
+            if in_range(h1):
+                head1_series(h1)
+            if in_range(h2):
+                head2_split(h2)
+            if in_range(h2 - 1):
+                head2_product(h2 - 1, nc.gpsimd if s < last_scores else nc.vector, 1)
+
+            for batch, pair in value_at.get(s + 1, ()):
+                group_values(batch, pair)
+
+            for batch, job in flip_at.get(s - 1, ()):
+                keep_flip(batch, job)
+            store((h1 - 2, h2 - 3))
+            for step in share_steps.get(s + 1, ()):
+                head2_differences(step)
             if in_range(s):
+                head2_late_difference(s)
                 head2_logit_pass0(s)
-            if values_due:
-                group_values(values_batch, pair)
-            if in_range(s - 2):
-                quantise_series("h2y0", s - 2, 2)
-                quantise_series("h2y1", s - 2, 2)
-                quantise_series("h2y2", s - 2, 2)
-            if values_due:
-                quantise_values(values_batch, pair)
-            if in_range(s - 1):
-                head2_product(s - 1, nc.vector, 2)
-
-            if in_range(s + SHARE_AHEAD):
-                head2_share1(s + SHARE_AHEAD)
-            if in_range(s):
-                head2_share2(s)
-            if in_range(s):
-                head1_series(s)
-            if in_range(s):
-                head2_split(s)
-            if in_range(s - 1):
-                head2_product(s - 1, nc.gpsimd, 1)
-
-            if flip_due:
-                keep_flip(flip_batch, job)
-            if in_range(s - 3):
-                store(s - 3)
-            if in_range(s + SCORES_AHEAD):
-                head2_differences(s + SCORES_AHEAD)
-            if (s + 1) % CHUNK == 0 and in_range(s + 1):
-                for step in range(s + 1, s + 1 + CHUNK):
+            for batch, job in flip_at.get(s, ()):
+                flip(batch, job)
+            if s + 1 in chunk_starts:
+                for step in range(s + 1, s + 1 + CHUNKS[chunk_starts.index(s + 1)]):
                     head2_log_share1(step)
+            for batch, job in flip_at.get(s + LOAD_AHEAD, ()):
+                load_flip(batch, job)
+            for batch, pair in value_at.get(s + LOAD_AHEAD, ()):
+                load_values(batch, pair)

@@ -29,14 +29,15 @@ QUERY_TILES = LENGTH // P
 BANK = P * PACK
 STEP = PASSES * BANK
 STEPS = BATCHES * QUERY_TILES
-CHUNKS = (2, 4, 4, 4, 4, 4, 4, 4, 2)
+CHUNKS = (2, 4, 6, 6, 6, 6, 2)
 CHUNK_BUFS = max(CHUNKS) + 2
 HEAD1_AHEAD = 4
 STORE_STEPS = 2
-FLIP_AHEAD = 13
+FLIP_AHEAD = 12
 VALUE_AT = (-HEAD1_AHEAD, 1 - HEAD1_AHEAD, 1, 2, 3)
 BANKS = 5
 SPLIT_LAG = 1
+SHARE_BUFS = 2
 LOAD_AHEAD = 2
 TINY = 2.0**-60
 
@@ -68,7 +69,7 @@ def tile_anomalyattention_pa_t_kernel(tc, q_plus, key_plus, retrieval, out):
         live = {}
 
         def load_keys(batch, pair):
-            raw = sb([P, PASSES, PACK, CHANNELS], BF16, "key_raw", 5)
+            raw = sb([P, PASSES, PACK, CHANNELS], BF16, "key_raw", 4)
             nc.sync.dma_start(
                 out=raw[:],
                 in_=key_plus[batch, pair].rearrange("(g p t) e -> p g t e", g=PASSES, t=PACK),
@@ -176,11 +177,11 @@ def tile_anomalyattention_pa_t_kernel(tc, q_plus, key_plus, retrieval, out):
         def head2_differences(step):
             d12 = sb([P, STEP], F32, "d12", CHUNK_BUFS + SPLIT_LAG)
             d01 = sb([P, BANK], F32, "d01", CHUNK_BUFS)
+            minus_s1 = score_bank("bank", BANKS, step, 1, 1, (3,))
+            a1 = sb([P, P, PACK], F32, "a1", 1)
+            nc.vector.tensor_scalar_mul(out=a1[:], in0=by_query(minus_s1), scalar1=-SCALE)
             s21 = score_bank("bank", BANKS, step, 1, 0, (3, 4))
             nc.vector.tensor_scalar_mul(out=half(d12, 0), in0=by_query(s21), scalar1=-SCALE)
-            minus_s1 = score_bank("bank", BANKS, step, 1, 1, (3,))
-            a1 = sb([P, P, PACK], F32, "a1", 2)
-            nc.vector.tensor_scalar_mul(out=a1[:], in0=by_query(minus_s1), scalar1=-SCALE)
             s2 = score_bank("bank", BANKS, step, 1, 1, (4,))
             s0 = score_bank("bank", BANKS, step, 1, 1, (2,))
             nc.vector.scalar_tensor_tensor(
@@ -221,15 +222,15 @@ def tile_anomalyattention_pa_t_kernel(tc, q_plus, key_plus, retrieval, out):
             nc.vector.tensor_tensor(out=half(logit, 1), in0=half(live["d01", step], 0), in1=half(logit, 1), op=ALU.add)
 
         def head2_share2(step):
-            share2 = sb([P, STEP], F32, "share2", 3)
+            share2 = sb([P, STEP], F32, "share2", SHARE_BUFS)
             nc.scalar.activation(out=share2[:], in_=live["d12", step][:], func=FUNC.Sigmoid, scale=-1.0)
             live["share2", step] = share2
 
         def head2_split(step):
             logit = live["logit", step]
-            y02 = sb([P, 2 * STEP], BF16, "h2y02", 3)
+            y02 = sb([P, 2 * STEP], BF16, "h2y02", 2)
             y0 = y02[:, :STEP]
-            rest = sb([P, STEP], F32, "rest", 3)
+            rest = sb([P, STEP], F32, "rest", SHARE_BUFS)
             nc.scalar.activation(out=y0, in_=logit[:], func=FUNC.Sigmoid)
             nc.scalar.activation(out=rest[:], in_=logit[:], func=FUNC.Sigmoid, scale=-1.0)
             live["h2y02", step] = y02
@@ -335,6 +336,7 @@ def tile_anomalyattention_pa_t_kernel(tc, q_plus, key_plus, retrieval, out):
                 else:
                     at = QUERY_TILES * batch - FLIP_AHEAD + (job - 3) % len(flips)
                 flip_at.setdefault(at, []).append((batch, job))
+        first_flips = [(0, job) for job in range(len(flips))]
         value_at = {}
         for batch in range(BATCHES):
             for pair in range(N_PAIRS):
@@ -346,8 +348,6 @@ def tile_anomalyattention_pa_t_kernel(tc, q_plus, key_plus, retrieval, out):
             h2 = s - SPLIT_LAG
             multiply((h1 - 2, h2 - 3))
 
-            if in_range(s):
-                head2_cap(s)
             if in_range(h1 - 1):
                 quantise_series("h1", 2, h1 - 1, 2)
             if in_range(s):
@@ -376,7 +376,8 @@ def tile_anomalyattention_pa_t_kernel(tc, q_plus, key_plus, retrieval, out):
                 group_values(batch, pair)
 
             for batch, job in flip_at.get(s - 1, ()):
-                keep_flip(batch, job)
+                if (batch, job) not in first_flips:
+                    keep_flip(batch, job)
             store((h1 - 2, h2 - 3))
             for step in share_steps.get(s + 1, ()):
                 head2_differences(step)
@@ -385,10 +386,18 @@ def tile_anomalyattention_pa_t_kernel(tc, q_plus, key_plus, retrieval, out):
                 head2_logit_pass0(s)
             for batch, job in flip_at.get(s, ()):
                 flip(batch, job)
+            for batch, job in flip_at.get(s, ()):
+                if (batch, job) in first_flips:
+                    keep_flip(batch, job)
             if s + 1 in chunk_starts:
                 for step in range(s + 1, s + 1 + CHUNKS[chunk_starts.index(s + 1)]):
                     head2_log_share1(step)
+                    head2_cap(step)
             for batch, job in flip_at.get(s + LOAD_AHEAD, ()):
-                load_flip(batch, job)
+                if batch == 0:
+                    load_flip(batch, job)
+            for batch, job in flip_at.get(s + 1, ()):
+                if batch > 0:
+                    load_flip(batch, job)
             for batch, pair in value_at.get(s + LOAD_AHEAD, ()):
                 load_values(batch, pair)

@@ -29,14 +29,15 @@ QUERY_TILES = LENGTH // P
 BANK = P * PACK
 STEP = PASSES * BANK
 STEPS = BATCHES * QUERY_TILES
-CHUNKS = (2, 4, 6, 6, 6, 6, 2)
+CHUNKS = (2, 4, 6, 7, 7, 6)
 CHUNK_BUFS = max(CHUNKS) + 2
 HEAD1_AHEAD = 4
-STORE_STEPS = 2
+STORE_STEPS = 1
 FLIP_AHEAD = 12
 VALUE_AT = (-HEAD1_AHEAD, 1 - HEAD1_AHEAD, 1, 2, 3)
 BANKS = 5
 SPLIT_LAG = 1
+RAWS = 6
 SHARE_BUFS = 2
 LOAD_AHEAD = 2
 TINY = 2.0**-60
@@ -69,7 +70,7 @@ def tile_anomalyattention_pa_t_kernel(tc, q_plus, key_plus, retrieval, out):
         live = {}
 
         def load_keys(batch, pair):
-            raw = sb([P, PASSES, PACK, CHANNELS], BF16, "key_raw", 4)
+            raw = sb([P, PASSES, PACK, CHANNELS], BF16, "raw", RAWS)
             nc.sync.dma_start(
                 out=raw[:],
                 in_=key_plus[batch, pair].rearrange("(g p t) e -> p g t e", g=PASSES, t=PACK),
@@ -93,18 +94,18 @@ def tile_anomalyattention_pa_t_kernel(tc, q_plus, key_plus, retrieval, out):
                 nc.vector.tensor_copy(out=keys_t[:], in_=flipped[:])
             live["keys_t", batch, pair] = keys_t
 
-        def load_queries(batch):
-            raw = sb([P, QUERY_TILES, 2, CHANNELS], BF16, "query_raw", 1)
+        def load_queries(batch, head):
+            raw = sb([P, QUERY_TILES, CHANNELS], BF16, "raw", RAWS)
             nc.sync.dma_start(
-                out=raw[:], in_=q_plus[batch].rearrange("(p i) x e -> p i x e", i=QUERY_TILES)
+                out=raw[:], in_=q_plus[batch].rearrange("(p i) x e -> p i x e", i=QUERY_TILES)[:, :, head, :]
             )
-            live["query_raw", batch] = raw
+            live["query_raw", batch, head] = raw
 
         def transpose_queries(batch, head):
-            raw = live["query_raw", batch]
+            raw = live["query_raw", batch, head]
             flipped = psum.tile([P, QUERY_TILES, P], BF16, name="bank", tag="bank", bufs=BANKS)
             for i in range(QUERY_TILES):
-                nc.tensor.transpose(out=flipped[:, i, :], in_=raw[:, i, head, :], identity=identity[:])
+                nc.tensor.transpose(out=flipped[:, i, :], in_=raw[:, i, :], identity=identity[:])
             live["flipped_queries", batch, head] = flipped
 
         def keep_queries(batch, head):
@@ -114,7 +115,7 @@ def tile_anomalyattention_pa_t_kernel(tc, q_plus, key_plus, retrieval, out):
             live["queries_t", batch, head] = queries_t
 
         def load_values(batch, pair):
-            raw = sb([P, PASSES, PACK, CHANNELS], BF16, "value_raw", 2)
+            raw = sb([P, PASSES, PACK, CHANNELS], BF16, "raw", RAWS)
             nc.sync.dma_start(
                 out=raw[:],
                 in_=retrieval[batch, pair].rearrange("(g p t) e -> p g t e", g=PASSES, t=PACK),
@@ -123,7 +124,7 @@ def tile_anomalyattention_pa_t_kernel(tc, q_plus, key_plus, retrieval, out):
 
         def group_values(batch, pair):
             raw = live["value_raw", batch, pair]
-            grouped = sb([P, PASSES, CHANNELS, PACK], BF16, "value_grouped", 2)
+            grouped = sb([P, PASSES, CHANNELS, PACK], BF16, "value_grouped", 1)
             nc.gpsimd.tensor_scalar(
                 out=grouped[:], in0=raw[:].rearrange("p g t e -> p g e t"), scalar1=1.0, scalar2=0.0,
                 op0=ALU.mult, op1=ALU.add,
@@ -132,8 +133,8 @@ def tile_anomalyattention_pa_t_kernel(tc, q_plus, key_plus, retrieval, out):
 
         def quantise_values(batch, pair):
             grouped = live["value_grouped", batch, pair]
-            codes = sb([P, PASSES * CHANNELS], U32, "value_codes%d" % pair, 2)
-            scales = sb([P, PASSES * CHANNELS], U8, "value_scales%d" % pair, 2)
+            codes = sb([P, PASSES * CHANNELS], U32, "value_codes", 7)
+            scales = sb([P, PASSES * CHANNELS], U8, "value_scales", 7)
             live["value_codes", batch, pair] = codes
             live["value_scales", batch, pair] = scales
             nc.vector.quantize_mx(
@@ -288,7 +289,10 @@ def tile_anomalyattention_pa_t_kernel(tc, q_plus, key_plus, retrieval, out):
                 live["result"] = sb([P, 2, STORE_STEPS, CHANNELS], F32, "result", 2)
             result = live["result"]
             xs = slice(made[0], made[-1] + 1)
-            nc.vector.tensor_copy(out=result[:, xs, slot, :], in_=live["product"][:, xs, :])
+            if steps[1] > STEPS - 10:
+                nc.scalar.copy(out=result[:, xs, slot, :], in_=live["product"][:, xs, :])
+            else:
+                nc.vector.tensor_copy(out=result[:, xs, slot, :], in_=live["product"][:, xs, :])
             if slot == STORE_STEPS - 1:
                 for x in made:
                     batch, i = divmod(steps[x], QUERY_TILES)
@@ -301,8 +305,8 @@ def tile_anomalyattention_pa_t_kernel(tc, q_plus, key_plus, retrieval, out):
             kind, index = flips[job]
             if kind == "keys":
                 load_keys(batch, index)
-            elif ("query_raw", batch) not in live:
-                load_queries(batch)
+            else:
+                load_queries(batch, index)
 
         def flip(batch, job):
             kind, index = flips[job]

@@ -29,15 +29,14 @@ QUERY_TILES = LENGTH // P
 BANK = P * PACK
 STEP = PASSES * BANK
 STEPS = BATCHES * QUERY_TILES
-CHUNKS = (2, 4, 6, 7, 7, 6)
+CHUNKS = (2, 3, 6, 7, 7, 7)
 CHUNK_BUFS = max(CHUNKS) + 2
 HEAD1_AHEAD = 4
 STORE_STEPS = 1
-FLIP_AHEAD = 12
-VALUE_AT = (-HEAD1_AHEAD, 1 - HEAD1_AHEAD, 1, 2, 3)
+FLIP_AHEAD = 14
 BANKS = 5
 SPLIT_LAG = 1
-RAWS = 6
+RAWS = 7
 SHARE_BUFS = 2
 LOAD_AHEAD = 2
 TINY = 2.0**-60
@@ -122,19 +121,23 @@ def tile_anomalyattention_pa_t_kernel(tc, q_plus, key_plus, retrieval, out):
             )
             live["value_raw", batch, pair] = raw
 
-        def group_values(batch, pair):
+        def group_values(batch, pair, g):
             raw = live["value_raw", batch, pair]
-            grouped = sb([P, PASSES, CHANNELS, PACK], BF16, "value_grouped", 1)
-            nc.gpsimd.tensor_scalar(
-                out=grouped[:], in0=raw[:].rearrange("p g t e -> p g e t"), scalar1=1.0, scalar2=0.0,
-                op0=ALU.mult, op1=ALU.add,
-            )
-            live["value_grouped", batch, pair] = grouped
+            if g == 0:
+                live["value_grouped", batch, pair] = sb([P, PASSES, CHANNELS, PACK], BF16, "value_grouped", 3)
+            grouped = live["value_grouped", batch, pair]
+            if pair == N_PAIRS - 1:
+                nc.vector.tensor_copy(out=grouped[:, g], in_=raw[:, g].rearrange("p t e -> p e t"))
+            else:
+                nc.gpsimd.tensor_scalar(
+                    out=grouped[:, g], in0=raw[:, g].rearrange("p t e -> p e t"), scalar1=1.0, scalar2=0.0,
+                    op0=ALU.mult, op1=ALU.add,
+                )
 
         def quantise_values(batch, pair):
             grouped = live["value_grouped", batch, pair]
-            codes = sb([P, PASSES * CHANNELS], U32, "value_codes", 7)
-            scales = sb([P, PASSES * CHANNELS], U8, "value_scales", 7)
+            codes = sb([P, PASSES * CHANNELS], U32, "value_codes", 9)
+            scales = sb([P, PASSES * CHANNELS], U8, "value_scales", 9)
             live["value_codes", batch, pair] = codes
             live["value_scales", batch, pair] = scales
             nc.vector.quantize_mx(
@@ -166,7 +169,7 @@ def tile_anomalyattention_pa_t_kernel(tc, q_plus, key_plus, retrieval, out):
             live[name + "_scales", step] = scales
 
         def head1_series(step):
-            both = sb([P, 2 * STEP], BF16, "h1", 2)
+            both = sb([P, 2 * STEP], BF16, "h1", 1)
             first = both[:, :STEP]
             second = both[:, STEP:]
             for g in range(PASSES):
@@ -176,8 +179,8 @@ def tile_anomalyattention_pa_t_kernel(tc, q_plus, key_plus, retrieval, out):
             live["h1", step] = both
 
         def head2_differences(step):
-            d12 = sb([P, STEP], F32, "d12", CHUNK_BUFS + SPLIT_LAG)
-            d01 = sb([P, BANK], F32, "d01", CHUNK_BUFS)
+            d12 = sb([P, STEP], F32, "d12", CHUNK_BUFS)
+            d01 = sb([P, BANK], F32, "d01", CHUNK_BUFS - 1)
             minus_s1 = score_bank("bank", BANKS, step, 1, 1, (3,))
             a1 = sb([P, P, PACK], F32, "a1", 1)
             nc.vector.tensor_scalar_mul(out=a1[:], in0=by_query(minus_s1), scalar1=-SCALE)
@@ -198,7 +201,7 @@ def tile_anomalyattention_pa_t_kernel(tc, q_plus, key_plus, retrieval, out):
             live["s01", step] = score_bank("bank", BANKS, step, 1, 0, (2, 3))
 
         def head2_share1(step):
-            share1 = sb([P, STEP], F32, "share1", CHUNK_BUFS + SPLIT_LAG)
+            share1 = sb([P, STEP], F32, "share1", CHUNK_BUFS + 1)
             nc.scalar.activation(out=share1[:], in_=live["d12", step][:], func=FUNC.Sigmoid)
             live["share1", step] = share1
 
@@ -232,8 +235,8 @@ def tile_anomalyattention_pa_t_kernel(tc, q_plus, key_plus, retrieval, out):
             y02 = sb([P, 2 * STEP], BF16, "h2y02", 2)
             y0 = y02[:, :STEP]
             rest = sb([P, STEP], F32, "rest", SHARE_BUFS)
-            nc.scalar.activation(out=y0, in_=logit[:], func=FUNC.Sigmoid)
             nc.scalar.activation(out=rest[:], in_=logit[:], func=FUNC.Sigmoid, scale=-1.0)
+            nc.scalar.activation(out=y0, in_=logit[:], func=FUNC.Sigmoid)
             live["h2y02", step] = y02
             live["rest", step] = rest
 
@@ -338,13 +341,21 @@ def tile_anomalyattention_pa_t_kernel(tc, q_plus, key_plus, retrieval, out):
                 if batch == 0:
                     at = -HEAD1_AHEAD - 2 if job < 3 else -HEAD1_AHEAD
                 else:
-                    at = QUERY_TILES * batch - FLIP_AHEAD + (job - 3) % len(flips)
+                    at = max(QUERY_TILES * batch - FLIP_AHEAD, -HEAD1_AHEAD) + (job - 3) % len(flips)
                 flip_at.setdefault(at, []).append((batch, job))
         first_flips = [(0, job) for job in range(len(flips))]
+        group_at = {}
         value_at = {}
+        load_at = {}
         for batch in range(BATCHES):
             for pair in range(N_PAIRS):
-                value_at.setdefault(QUERY_TILES * batch + VALUE_AT[pair], []).append((batch, pair))
+                for g in range(PASSES):
+                    at = QUERY_TILES * batch - 9 + PASSES * pair + (g if pair < 4 else 0)
+                    at = max(at, -HEAD1_AHEAD - 1)
+                    group_at.setdefault(at, []).append((batch, pair, g))
+                    if g == 0:
+                        load_at.setdefault(at - LOAD_AHEAD, []).append((batch, pair))
+                value_at.setdefault(at + 1, []).append((batch, pair))
 
         last_scores = max(share_steps)
         for s in range(-HEAD1_AHEAD - 2 - LOAD_AHEAD, STEPS + 4 + SPLIT_LAG):
@@ -376,8 +387,8 @@ def tile_anomalyattention_pa_t_kernel(tc, q_plus, key_plus, retrieval, out):
             if in_range(h2 - 1):
                 head2_product(h2 - 1, nc.gpsimd if s < last_scores else nc.vector, 1)
 
-            for batch, pair in value_at.get(s + 1, ()):
-                group_values(batch, pair)
+            for batch, pair, g in group_at.get(s, ()):
+                group_values(batch, pair, g)
 
             for batch, job in flip_at.get(s - 1, ()):
                 if (batch, job) not in first_flips:
@@ -403,5 +414,5 @@ def tile_anomalyattention_pa_t_kernel(tc, q_plus, key_plus, retrieval, out):
             for batch, job in flip_at.get(s + 1, ()):
                 if batch > 0:
                     load_flip(batch, job)
-            for batch, pair in value_at.get(s + LOAD_AHEAD, ()):
+            for batch, pair in load_at.get(s, ()):
                 load_values(batch, pair)

@@ -66,6 +66,25 @@ def tile_anomalyattention_pa_t_kernel(tc, q_plus, key_plus, retrieval, out):
         tiny = sb([P, 1], F32, "tiny", 1)
         nc.vector.memset(tiny[:], TINY)
 
+        ones = sb([P, P * PACK], BF16, "ones", 1)
+        nc.vector.memset(ones[:], 1.0)
+        warm_codes = sb([P, P], U32, "warm_codes", 1)
+        warm_scales = sb([P, P], U8, "warm_scales", 1)
+        nc.vector.quantize_mx(out=warm_codes[:].bitcast(FP8X4), scales=warm_scales[:], in_=ones[:])
+
+        def keep_warm(count):
+            bank = psum.tile([P, P], F32, name="product", tag="product", bufs=1)
+            for n in range(count):
+                nc.tensor.matmul_mx(
+                    out=bank[:],
+                    lhsT=warm_codes[:].bitcast(FP8X4),
+                    lhsT_scale=warm_scales[:],
+                    rhs=warm_codes[:].bitcast(FP8X4),
+                    rhs_scale=warm_scales[:],
+                    start=True,
+                    stop=True,
+                )
+
         live = {}
 
         def load_keys(batch, pair):
@@ -400,6 +419,8 @@ def tile_anomalyattention_pa_t_kernel(tc, q_plus, key_plus, retrieval, out):
                 head2_late_difference(s)
                 head2_logit_pass0(s)
             for batch, job in flip_at.get(s, ()):
+                if (batch, job) == (0, 0):
+                    keep_warm(16)
                 flip(batch, job)
             for batch, job in flip_at.get(s, ()):
                 if (batch, job) in first_flips:

@@ -311,7 +311,7 @@ def tile_anomalyattention_pa_t_kernel(tc, q_plus, key_plus, retrieval, out):
                 live["result"] = sb([P, 2, STORE_STEPS, CHANNELS], F32, "result", 2)
             result = live["result"]
             xs = slice(made[0], made[-1] + 1)
-            if steps[1] > STEPS - 10:
+            if steps[1] > STEPS - 9:
                 nc.scalar.copy(out=result[:, xs, slot, :], in_=live["product"][:, xs, :])
             else:
                 nc.vector.tensor_copy(out=result[:, xs, slot, :], in_=live["product"][:, xs, :])
@@ -354,6 +354,7 @@ def tile_anomalyattention_pa_t_kernel(tc, q_plus, key_plus, retrieval, out):
             for j in range(size):
                 share_steps.setdefault(chunk_starts[n] - before + j * before // size, []).append(chunk_starts[n] + j)
 
+        to_cap = []
         flip_at = {}
         for batch in range(BATCHES):
             for job in range(len(flips)):
@@ -384,14 +385,17 @@ def tile_anomalyattention_pa_t_kernel(tc, q_plus, key_plus, retrieval, out):
 
             if in_range(h1 - 1):
                 quantise_series("h1", 2, h1 - 1, 2)
-            if in_range(s):
-                head2_logit_pass1(s)
             if in_range(h2 - 2):
                 quantise_series("h2y02", 2, h2 - 2, 2)
             for batch, pair in value_at.get(s, ()):
                 quantise_values(batch, pair)
             if in_range(h2 - 1):
                 head2_product(h2 - 1, nc.vector, 2)
+            for step in to_cap:
+                head2_cap(step)
+            to_cap.clear()
+            if in_range(s):
+                head2_logit_pass1(s)
             if in_range(h2 - 2):
                 quantise_series("h2y1", 1, h2 - 2, 2)
 
@@ -428,7 +432,7 @@ def tile_anomalyattention_pa_t_kernel(tc, q_plus, key_plus, retrieval, out):
             if s + 1 in chunk_starts:
                 for step in range(s + 1, s + 1 + CHUNKS[chunk_starts.index(s + 1)]):
                     head2_log_share1(step)
-                    head2_cap(step)
+                    to_cap.append(step)
             for batch, job in flip_at.get(s + LOAD_AHEAD, ()):
                 if batch == 0:
                     load_flip(batch, job)

import math
from contextlib import ExitStack

import concourse.mybir as mybir
from concourse.masks import make_identity

F32 = mybir.dt.float32
BF16 = mybir.dt.bfloat16
U32 = mybir.dt.uint32
U8 = mybir.dt.uint8
FP8X4 = mybir.dt.float8_e4m3fn_x4
FUNC = mybir.ActivationFunctionType
ALU = mybir.AluOpType

BATCHES = 4
LENGTH = 1024
CHANNELS = 128
N_PAIRS = 5
HEAD1_PAIRS = (0, 1)
HEAD2_PAIRS = (2, 3, 4)
LATE_PAIRS = (2, 3)
NEGATED_PAIRS = (1, 3)
SCALE = 1.0 / math.sqrt(CHANNELS)

P = 128
PACK = 4
PASSES = LENGTH // (P * PACK)
QUERY_TILES = LENGTH // P
BANK = P * PACK
STEP = PASSES * BANK
STEPS = BATCHES * QUERY_TILES
CHUNKS = (2, 3, 6, 7, 7, 7)
CHUNK_BUFS = max(CHUNKS) + 2
HEAD1_AHEAD = 4
STORE_STEPS = 1
FLIP_AHEAD = 14
BANKS = 5
SPLIT_LAG = 1
RAWS = 7
SHARE_BUFS = 2
LOAD_AHEAD = 2
TINY = 2.0**-60

FLOPS = 2 * 2 * BATCHES * N_PAIRS * LENGTH * LENGTH * CHANNELS


def tile_anomalyattention_pa_t_kernel(tc, q_plus, key_plus, retrieval, out):
    nc = tc.nc
    stack = ExitStack()
    with stack:
        sbuf = stack.enter_context(tc.tile_pool(name="sbuf", bufs=1))
        psum = stack.enter_context(tc.psum_pool(name="psum", bufs=1))
        stack.enter_context(tc.manual_schedule())

        def sb(shape, dtype, tag, bufs):
            return sbuf.tile(shape, dtype, name=tag, tag=tag, bufs=bufs, align_bytes=64)

        def by_query(bank):
            return bank[:].rearrange("p t l -> p l t")

        def half(tile, g):
            return tile[:, g * BANK : (g + 1) * BANK].rearrange("p (l t) -> p l t", t=PACK)

        identity = sb([P, P], BF16, "identity", 1)
        make_identity(nc, identity[:])
        tiny = sb([P, 1], F32, "tiny", 1)
        nc.vector.memset(tiny[:], TINY)

        ones = sb([P, P * PACK], BF16, "ones", 1)
        nc.vector.memset(ones[:], 1.0)
        warm_codes = sb([P, P], U32, "warm_codes", 1)
        warm_scales = sb([P, P], U8, "warm_scales", 1)
        nc.vector.quantize_mx(out=warm_codes[:].bitcast(FP8X4), scales=warm_scales[:], in_=ones[:])

        def keep_warm(count):
            bank = psum.tile([P, P], F32, name="product", tag="product", bufs=1)
            for n in range(count):
                nc.tensor.matmul_mx(
                    out=bank[:],
                    lhsT=warm_codes[:].bitcast(FP8X4),
                    lhsT_scale=warm_scales[:],
                    rhs=warm_codes[:].bitcast(FP8X4),
                    rhs_scale=warm_scales[:],
                    start=True,
                    stop=True,
                )

        live = {}

        def load_keys(batch, pair):
            raw = sb([P, PASSES, PACK, CHANNELS], BF16, "raw", RAWS)
            nc.sync.dma_start(
                out=raw[:],
                in_=key_plus[batch, pair].rearrange("(g p t) e -> p g t e", g=PASSES, t=PACK),
            )
            live["key_raw", batch, pair] = raw

        def transpose_keys(batch, pair):
            raw = live["key_raw", batch, pair]
            flipped = psum.tile([P, PASSES, PACK, P], BF16, name="bank", tag="bank", bufs=BANKS)
            for g in range(PASSES):
                for t in range(PACK):
                    nc.tensor.transpose(out=flipped[:, g, t, :], in_=raw[:, g, t, :], identity=identity[:])
            live["flipped_keys", batch, pair] = flipped

        def keep_keys(batch, pair):
            flipped = live["flipped_keys", batch, pair]
            keys_t = sb([P, PASSES, PACK, P], BF16, "keys_t%d" % pair, 3 if pair in LATE_PAIRS else 2)
            if pair in NEGATED_PAIRS:
                nc.vector.tensor_scalar_mul(out=keys_t[:], in0=flipped[:], scalar1=-1.0)
            else:
                nc.vector.tensor_copy(out=keys_t[:], in_=flipped[:])
            live["keys_t", batch, pair] = keys_t

        def load_queries(batch, head):
            raw = sb([P, QUERY_TILES, CHANNELS], BF16, "raw", RAWS)
            nc.sync.dma_start(
                out=raw[:], in_=q_plus[batch].rearrange("(p i) x e -> p i x e", i=QUERY_TILES)[:, :, head, :]
            )
            live["query_raw", batch, head] = raw

        def transpose_queries(batch, head):
            raw = live["query_raw", batch, head]
            flipped = psum.tile([P, QUERY_TILES, P], BF16, name="bank", tag="bank", bufs=BANKS)
            for i in range(QUERY_TILES):
                nc.tensor.transpose(out=flipped[:, i, :], in_=raw[:, i, :], identity=identity[:])
            live["flipped_queries", batch, head] = flipped

        def keep_queries(batch, head):
            flipped = live["flipped_queries", batch, head]
            queries_t = sb([P, QUERY_TILES, P], BF16, "queries_t%d" % head, 2 + head)
            nc.vector.tensor_copy(out=queries_t[:], in_=flipped[:])
            live["queries_t", batch, head] = queries_t

        def load_values(batch, pair):
            raw = sb([P, PASSES, PACK, CHANNELS], BF16, "raw", RAWS)
            nc.sync.dma_start(
                out=raw[:],
                in_=retrieval[batch, pair].rearrange("(g p t) e -> p g t e", g=PASSES, t=PACK),
            )
            live["value_raw", batch, pair] = raw

        def group_values(batch, pair, g):
            raw = live["value_raw", batch, pair]
            if g == 0:
                live["value_grouped", batch, pair] = sb([P, PASSES, CHANNELS, PACK], BF16, "value_grouped", 3)
            grouped = live["value_grouped", batch, pair]
            if pair == N_PAIRS - 1:
                nc.vector.tensor_copy(out=grouped[:, g], in_=raw[:, g].rearrange("p t e -> p e t"))
            else:
                nc.gpsimd.tensor_scalar(
                    out=grouped[:, g], in0=raw[:, g].rearrange("p t e -> p e t"), scalar1=1.0, scalar2=0.0,
                    op0=ALU.mult, op1=ALU.add,
                )

        def quantise_values(batch, pair):
            grouped = live["value_grouped", batch, pair]
            codes = sb([P, PASSES * CHANNELS], U32, "value_codes", 9)
            scales = sb([P, PASSES * CHANNELS], U8, "value_scales", 9)
            live["value_codes", batch, pair] = codes
            live["value_scales", batch, pair] = scales
            nc.vector.quantize_mx(
                out=codes[:].bitcast(FP8X4),
                scales=scales[:],
                in_=grouped[:].rearrange("p g e t -> p (g e t)"),
            )

        def score_bank(tag, bufs, step, head, g, pairs):
            batch, i = divmod(step, QUERY_TILES)
            bank = psum.tile([P, PACK, P], F32, name=tag, tag=tag, bufs=bufs)
            for t in range(PACK):
                for j, pair in enumerate(pairs):
                    nc.tensor.matmul(
                        out=bank[:, t, :],
                        lhsT=live["keys_t", batch, pair][:, g, t, :],
                        rhs=live["queries_t", batch, head][:, i, :],
                        start=(j == 0),
                        stop=(j == len(pairs) - 1),
                    )
            return bank

        def quantise_series(name, count, step, bufs):
            series = live[name, step]
            codes = sb([P, count * PASSES * P], U32, name + "_codes", bufs)
            scales = sb([P, count * PASSES * P], U8, name + "_scales", bufs)
            nc.vector.quantize_mx(out=codes[:].bitcast(FP8X4), scales=scales[:], in_=series[:])
            live[name + "_codes", step] = codes
            live[name + "_scales", step] = scales

        def head1_series(step):
            both = sb([P, 2 * STEP], BF16, "h1", 1)
            first = both[:, :STEP]
            second = both[:, STEP:]
            for g in range(PASSES):
                gap = score_bank("gap", 2, step, 0, g, (0, 1))
                nc.scalar.activation(out=half(first, g), in_=by_query(gap), func=FUNC.Sigmoid, scale=SCALE)
                nc.scalar.activation(out=half(second, g), in_=by_query(gap), func=FUNC.Sigmoid, scale=-SCALE)
            live["h1", step] = both

        def head2_differences(step):
            d12 = sb([P, STEP], F32, "d12", CHUNK_BUFS)
            d01 = sb([P, BANK], F32, "d01", CHUNK_BUFS - 1)
            minus_s1 = score_bank("bank", BANKS, step, 1, 1, (3,))
            a1 = sb([P, P, PACK], F32, "a1", 1)
            nc.vector.tensor_scalar_mul(out=a1[:], in0=by_query(minus_s1), scalar1=-SCALE)
            s21 = score_bank("bank", BANKS, step, 1, 0, (3, 4))
            nc.vector.tensor_scalar_mul(out=half(d12, 0), in0=by_query(s21), scalar1=-SCALE)
            s2 = score_bank("bank", BANKS, step, 1, 1, (4,))
            s0 = score_bank("bank", BANKS, step, 1, 1, (2,))
            nc.vector.scalar_tensor_tensor(
                out=half(d12, 1), in0=by_query(s2), scalar=-SCALE, in1=a1[:], op0=ALU.mult, op1=ALU.add
            )
            nc.vector.scalar_tensor_tensor(
                out=half(d01, 0), in0=by_query(s0), scalar=SCALE, in1=a1[:], op0=ALU.mult, op1=ALU.subtract
            )
            live["d12", step] = d12
            live["d01", step] = d01

        def head2_late_difference(step):
            live["s01", step] = score_bank("bank", BANKS, step, 1, 0, (2, 3))

        def head2_share1(step):
            share1 = sb([P, STEP], F32, "share1", CHUNK_BUFS + 1)
            nc.scalar.activation(out=share1[:], in_=live["d12", step][:], func=FUNC.Sigmoid)
            live["share1", step] = share1

        def head2_log_share1(step):
            logit = sb([P, STEP], F32, "logit", max(CHUNKS) + SPLIT_LAG)
            nc.scalar.activation(out=logit[:], in_=live["share1", step][:], func=FUNC.Ln, bias=tiny[:])
            live["logit", step] = logit

        def head2_cap(step):
            logit = live["logit", step]
            nc.vector.tensor_tensor(out=logit[:], in0=live["d12", step][:], in1=logit[:], op=ALU.min)

        def head2_logit_pass0(step):
            logit = live["logit", step]
            nc.vector.scalar_tensor_tensor(
                out=half(logit, 0), in0=by_query(live["s01", step]), scalar=SCALE, in1=half(logit, 0),
                op0=ALU.mult, op1=ALU.add,
            )

        def head2_logit_pass1(step):
            logit = live["logit", step]
            nc.vector.tensor_tensor(out=half(logit, 1), in0=half(live["d01", step], 0), in1=half(logit, 1), op=ALU.add)

        def head2_share2(step):
            share2 = sb([P, STEP], F32, "share2", SHARE_BUFS)
            nc.scalar.activation(out=share2[:], in_=live["d12", step][:], func=FUNC.Sigmoid, scale=-1.0)
            live["share2", step] = share2

        def head2_split(step):
            logit = live["logit", step]
            y02 = sb([P, 2 * STEP], BF16, "h2y02", 2)
            y0 = y02[:, :STEP]
            rest = sb([P, STEP], F32, "rest", SHARE_BUFS)
            nc.scalar.activation(out=rest[:], in_=logit[:], func=FUNC.Sigmoid, scale=-1.0)
            nc.scalar.activation(out=y0, in_=logit[:], func=FUNC.Sigmoid)
            live["h2y02", step] = y02
            live["rest", step] = rest

        def head2_product(step, engine, y):
            if y == 1:
                tile = sb([P, STEP], BF16, "h2y1", 1)
                live["h2y1", step] = tile
                product = tile[:]
            else:
                product = live["h2y02", step][:, STEP:]
            engine.tensor_tensor(
                out=product, in0=live["rest", step][:], in1=live["share%d" % y, step][:], op=ALU.mult
            )

        heads = (
            ((("h1", 0), ("h1", 1)), HEAD1_PAIRS),
            ((("h2y02", 0), ("h2y1", 0), ("h2y02", 1)), HEAD2_PAIRS),
        )

        def multiply(steps):
            if not any(in_range(step) for step in steps):
                return
            product = psum.tile([P, 2, CHANNELS], F32, name="product", tag="product", bufs=1)
            for x, (names, pairs) in enumerate(heads):
                step = steps[x]
                if not in_range(step):
                    continue
                batch = step // QUERY_TILES
                last = len(names) * PASSES - 1
                for y, ((name, place), pair) in enumerate(zip(names, pairs)):
                    codes = live[name + "_codes", step]
                    scales = live[name + "_scales", step]
                    for g in range(PASSES):
                        cols = slice(g * P, (g + 1) * P)
                        series_cols = slice((place * PASSES + g) * P, (place * PASSES + g + 1) * P)
                        nc.tensor.matmul_mx(
                            out=product[:, x, :],
                            lhsT=codes[:, series_cols].bitcast(FP8X4),
                            lhsT_scale=scales[:, series_cols],
                            rhs=live["value_codes", batch, pair][:, cols].bitcast(FP8X4),
                            rhs_scale=live["value_scales", batch, pair][:, cols],
                            start=(y * PASSES + g == 0),
                            stop=(y * PASSES + g == last),
                        )
            live["product"] = product

        def store(steps):
            made = [x for x in range(2) if in_range(steps[x])]
            if not made:
                return
            slot = steps[0] % STORE_STEPS
            if slot == 0:
                live["result"] = sb([P, 2, STORE_STEPS, CHANNELS], F32, "result", 2)
            result = live["result"]
            xs = slice(made[0], made[-1] + 1)
            if steps[1] > STEPS - 9:
                nc.scalar.copy(out=result[:, xs, slot, :], in_=live["product"][:, xs, :])
            else:
                nc.vector.tensor_copy(out=result[:, xs, slot, :], in_=live["product"][:, xs, :])
            if slot == STORE_STEPS - 1:
                for x in made:
                    batch, i = divmod(steps[x], QUERY_TILES)
                    rows = out[batch].rearrange("(p i) x e -> p i x e", i=QUERY_TILES)
                    nc.sync.dma_start(out=rows[:, i + 1 - STORE_STEPS : i + 1, x, :], in_=result[:, x, :, :])

        flips = [("keys", 0), ("keys", 1), ("queries", 0), ("keys", 3), ("keys", 4), ("queries", 1), ("keys", 2)]

        def load_flip(batch, job):
            kind, index = flips[job]
            if kind == "keys":
                load_keys(batch, index)
            else:
                load_queries(batch, index)

        def flip(batch, job):
            kind, index = flips[job]
            if kind == "keys":
                transpose_keys(batch, index)
            else:
                transpose_queries(batch, index)

        def keep_flip(batch, job):
            kind, index = flips[job]
            if kind == "keys":
                keep_keys(batch, index)
            else:
                keep_queries(batch, index)

        def in_range(step):
            return 0 <= step < STEPS

        chunk_starts = [sum(CHUNKS[:n]) for n in range(len(CHUNKS))]
        share_steps = {}
        for n, size in enumerate(CHUNKS):
            before = CHUNKS[max(n - 1, 0)]
            for j in range(size):
                share_steps.setdefault(chunk_starts[n] - before + j * before // size, []).append(chunk_starts[n] + j)

        to_cap = []
        flip_at = {}
        for batch in range(BATCHES):
            for job in range(len(flips)):
                if batch == 0:
                    at = -HEAD1_AHEAD - 2 if job < 3 else -HEAD1_AHEAD
                else:
                    at = max(QUERY_TILES * batch - FLIP_AHEAD, -HEAD1_AHEAD) + (job - 3) % len(flips)
                flip_at.setdefault(at, []).append((batch, job))
        first_flips = [(0, job) for job in range(len(flips))]
        group_at = {}
        value_at = {}
        load_at = {}
        for batch in range(BATCHES):
            for pair in range(N_PAIRS):
                for g in range(PASSES):
                    at = QUERY_TILES * batch - 9 + PASSES * pair + (g if pair < 4 else 0)
                    at = max(at, -HEAD1_AHEAD - 1)
                    group_at.setdefault(at, []).append((batch, pair, g))
                    if g == 0:
                        load_at.setdefault(at - LOAD_AHEAD, []).append((batch, pair))
                value_at.setdefault(at + 1, []).append((batch, pair))

        last_scores = max(share_steps)
        for s in range(-HEAD1_AHEAD - 2 - LOAD_AHEAD, STEPS + 4 + SPLIT_LAG):
            h1 = s + HEAD1_AHEAD
            h2 = s - SPLIT_LAG
            multiply((h1 - 2, h2 - 3))

            if in_range(h1 - 1):
                quantise_series("h1", 2, h1 - 1, 2)
            if in_range(h2 - 2):
                quantise_series("h2y02", 2, h2 - 2, 2)
            for batch, pair in value_at.get(s, ()):
                quantise_values(batch, pair)
            if in_range(h2 - 1):
                head2_product(h2 - 1, nc.vector, 2)
            for step in to_cap:
                head2_cap(step)
            to_cap.clear()
            if in_range(s):
                head2_logit_pass1(s)
            if in_range(h2 - 2):
                quantise_series("h2y1", 1, h2 - 2, 2)

            for step in share_steps.get(s, ()):
                head2_share1(step)
            if in_range(h2):
                head2_share2(h2)
            if in_range(h1):
                head1_series(h1)
            if in_range(h2):
                head2_split(h2)
            if in_range(h2 - 1):
                head2_product(h2 - 1, nc.gpsimd if s < last_scores else nc.vector, 1)

            for batch, pair, g in group_at.get(s, ()):
                group_values(batch, pair, g)

            for batch, job in flip_at.get(s - 1, ()):
                if (batch, job) not in first_flips:
                    keep_flip(batch, job)
            store((h1 - 2, h2 - 3))
            for step in share_steps.get(s + 1, ()):
                head2_differences(step)
            if in_range(s):
                head2_late_difference(s)
                head2_logit_pass0(s)
            for batch, job in flip_at.get(s, ()):
                if (batch, job) == (0, 0):
                    keep_warm(16)
                flip(batch, job)
            for batch, job in flip_at.get(s, ()):
                if (batch, job) in first_flips:
                    keep_flip(batch, job)
            if s + 1 in chunk_starts:
                for step in range(s + 1, s + 1 + CHUNKS[chunk_starts.index(s + 1)]):
                    head2_log_share1(step)
                    to_cap.append(step)
            for batch, job in flip_at.get(s + LOAD_AHEAD, ()):
                if batch == 0:
                    load_flip(batch, job)
            for batch, job in flip_at.get(s + 1, ()):
                if batch > 0:
                    load_flip(batch, job)
            for batch, pair in load_at.get(s, ()):
                load_values(batch, pair)
